import numpy as np
import ml_dtypes


def mxq(x, axis, fmt="e4m3"):
    dtype, down = {"e4m3": (ml_dtypes.float8_e4m3fn, 7), "e5m2": (ml_dtypes.float8_e5m2, 14)}[fmt]
    v = np.moveaxis(np.asarray(x, np.float32).astype(ml_dtypes.bfloat16).astype(np.float64), axis, -1)
    blocks = v.reshape(v.shape[:-1] + (-1, 32))
    amax = np.abs(blocks).max(-1, keepdims=True)
    byte = np.maximum(np.where(amax > 0, np.frexp(amax)[1] - 1 + 127, 0) - down, 1)
    scale = np.exp2(byte - 127.0)
    codes = (blocks / scale).astype(np.float32).astype(dtype).astype(np.float64)
    return np.moveaxis((codes * scale).reshape(v.shape), -1, axis)


WIDE = False


def mx_kscale(k):
    if not WIDE:
        return np.ones(k)
    levels = np.array([10, -10, 5, -5, 0])
    if k % 512:
        return np.exp2(np.random.permutation(np.resize(levels, k // 32))).repeat(32)
    a = np.empty((k // 512, 16))
    for p in range(k // 512):
        a[p, :8] = np.random.permutation(np.resize(levels, 8))
        for g in range(8):
            far = levels[np.abs(levels - a[p, g]) >= 10]
            a[p, g + 8] = far[np.random.randint(len(far))]
    return np.exp2(a.ravel()).repeat(32)


BF16 = ml_dtypes.bfloat16


def bf(x):
    return np.asarray(x, np.float32).astype(BF16)


def f64(x):
    return np.asarray(x).astype(np.float64)


B, N, SIZE, CH = 256, 16, 1024, 512


def sigmoid(v):
    return 1.0 / (1.0 + np.exp(-v))


def setup_inputs():
    s = mx_kscale(SIZE)
    d = {"z0": bf(np.random.standard_normal((B, SIZE)) * s),
         "h_tilde": bf(np.random.standard_normal((B, CH)) * np.sqrt(N)),
         "fc_sum": bf(np.random.standard_normal((B, CH)) * 1.2)}
    for g in ("i", "o", "u"):
        d["W_" + g] = bf(np.random.standard_normal((CH, SIZE)) / np.sqrt(SIZE) / s)
        d["U_" + g] = bf(np.random.standard_normal((CH, CH)) / np.sqrt(CH * N))
        d["b_" + g] = bf(np.random.standard_normal(CH) * 0.5)
    return d


def core(z0, h_tilde, fc_sum, W_i, U_i, b_i, W_o, U_o, b_o, W_u, U_u, b_u):
    zq = mxq(f64(z0), 1, "e4m3")
    ht = f64(h_tilde)
    i_j = sigmoid((zq @ mxq(f64(W_i), 1, "e4m3").T) + ht @ f64(U_i).T + f64(b_i))
    o_j = sigmoid((zq @ mxq(f64(W_o), 1, "e4m3").T) + ht @ f64(U_o).T + f64(b_o))
    u_j = np.tanh((zq @ mxq(f64(W_u), 1, "e4m3").T) + ht @ f64(U_u).T + f64(b_u))
    c_j = i_j * u_j + f64(fc_sum)
    h_j = o_j * np.tanh(c_j)
    return np.concatenate([h_j, c_j], axis=-1)


def e4m3fn_bytes(y):
    return np.clip(np.asarray(y, np.float64), -448.0, 448.0).astype(np.float32).astype(ml_dtypes.float8_e4m3fn).view(np.uint8)


def reference(z0, h_tilde, fc_sum, W_i, U_i, b_i, W_o, U_o, b_o, W_u, U_u, b_u):
    out = core(z0, h_tilde, fc_sum, W_i, U_i, b_i, W_o, U_o, b_o, W_u, U_u, b_u)
    s = np.max(np.abs(out), axis=-1, keepdims=True) / 448.0
    return out, e4m3fn_bytes(out / s)

@@ -1,0 +1,336 @@
+from contextlib import ExitStack
+
+import concourse.mybir as mybir
+from concourse.masks import make_identity
+
+B, SIZE, CH = 256, 1024, 512
+FLOPS = 2 * B * (3 * CH) * (SIZE + CH)
+
+F32 = mybir.dt.float32
+BF16 = mybir.dt.bfloat16
+U32 = mybir.dt.uint32
+U8 = mybir.dt.uint8
+FP8X4 = mybir.dt.float8_e4m3fn_x4
+FP8 = mybir.dt.float8_e4m3fn
+ACT = mybir.ActivationFunctionType
+ALU = mybir.AluOpType
+AX = mybir.AxisListType
+
+P = 128
+MT = B // P
+KT = CH // P
+NPASS = SIZE // 512
+NB = 2
+N = NB * P
+NA = 4
+NS = 6
+
+
+def tile_treelstm_pb_kernel(
+    tc, z0, h_tilde, fc_sum, W_i, U_i, b_i, W_o, U_o, b_o, W_u, U_u, b_u, out_0, out_1
+):
+    nc = tc.nc
+    out0v = out_0.rearrange("(m p) n -> p m n", p=P)
+    out1v = out_1.rearrange("(m p) n -> p m n", p=P)
+
+    with ExitStack() as ctx:
+        const = ctx.enter_context(tc.tile_pool(name="const", bufs=1))
+        inp = ctx.enter_context(tc.tile_pool(name="inp", bufs=1))
+        keep = ctx.enter_context(tc.tile_pool(name="keep", bufs=1))
+        ep = ctx.enter_context(tc.tile_pool(name="ep", bufs=3))
+        psT = ctx.enter_context(tc.psum_pool(name="psT", bufs=4))
+        psP = ctx.enter_context(tc.psum_pool(name="psP", bufs=2))
+        psX = ctx.enter_context(tc.psum_pool(name="psX", bufs=2))
+
+        bias_row = const.tile([P, 3 * CH], BF16, name="bias_row")
+        nc.vector.memset(bias_row[:], 0.0)
+        for j, b in enumerate((b_i, b_u, b_o)):
+            nc.scalar.dma_start(
+                out=bias_row[0:1, j * CH : (j + 1) * CH], in_=b.rearrange("(o c) -> o c", o=1)
+            )
+        ones = const.tile([P, P], BF16, name="ones")
+        nc.vector.memset(ones[:], 1.0)
+        zcol = const.tile([P, 1], F32, name="zcol")
+        nc.vector.memset(zcol[:], 0.0)
+        warm = const.tile([P, 1], F32, name="warm")
+        nc.scalar.activation(out=warm[:], in_=zcol[:], func=ACT.Sigmoid)
+        ident_b = const.tile([P, P], BF16, name="ident_b")
+        make_identity(nc, ident_b[:])
+        ident_f = const.tile([P, P], F32, name="ident_f")
+        make_identity(nc, ident_f[:])
+
+        def load_rows(dram, r0, nrt, width, name):
+            t = inp.tile([P, nrt, width], BF16, name=name)
+            nc.sync.dma_start(
+                out=t[:], in_=dram[r0 * P : (r0 + nrt) * P, :].rearrange("(t p) k -> p t k", p=P)
+            )
+            return [t[:, j, :] for j in range(nrt)]
+
+        u_in = {}
+        w_in = {}
+        h_in = load_rows(h_tilde, 0, 1, CH, "h_in0") + load_rows(h_tilde, 1, 1, CH, "h_in1")
+        u_in[0] = load_rows(U_i, 0, 1, CH, "Ui0") + load_rows(U_u, 0, 1, CH, "Uu0")
+        z_in = load_rows(z0, 0, 1, SIZE, "z_in0") + load_rows(z0, 1, 1, SIZE, "z_in1")
+        fc_sb = inp.tile([P, MT, CH], BF16, name="fc_sb")
+        for k in range(NA):
+            w_in[k] = load_rows(W_i, k, 1, SIZE, "Wi%d" % k) + load_rows(W_u, k, 1, SIZE, "Wu%d" % k)
+            if k >= 1:
+                u_in[k] = load_rows(U_i, k, 1, CH, "Ui%d" % k) + load_rows(U_u, k, 1, CH, "Uu%d" % k)
+            if k == 2:
+                nc.sync.dma_start(out=fc_sb[:], in_=fc_sum.rearrange("(m p) c -> p m c", p=P))
+        w_in[NA] = load_rows(W_o, 0, NB, SIZE, "Wo0")
+        u_o = load_rows(U_o, 0, 2 * NB, CH, "Uo")
+        u_in[NA] = u_o[0:NB]
+        u_in[NA + 1] = u_o[NB : 2 * NB]
+        w_in[NA + 1] = load_rows(W_o, NB, NB, SIZE, "Wo1")
+
+        hT = keep.tile([P, KT, MT, P], BF16, name="hT")
+        zgr = [keep.tile([P, NPASS * P * 4], BF16, name="zgr%d" % m, align_bytes=64) for m in range(MT)]
+        zc = keep.tile([P, MT * NPASS * P], U32, name="zc", align_bytes=64)
+        zs = keep.tile([P, MT * NPASS * P], U8, name="zs", align_bytes=64)
+        bias_sb = keep.tile([P, 2, CH], F32, name="bias_sb")
+        c_sb = keep.tile([P, MT, CH], F32, name="c_sb")
+        tch = keep.tile([P, MT, CH], F32, name="tch")
+        h_sb = keep.tile([P, MT, CH], F32, name="h_sb")
+        pmx = keep.tile([P, 3, MT], F32, name="pmx")
+        mab = keep.tile([P, MT], F32, name="mab")
+        sab = keep.tile([P, MT], F32, name="sab")
+        sc = keep.tile([P, MT], F32, name="sc")
+        rs = keep.tile([P, MT], F32, name="rs")
+        qc = keep.tile([P, MT, CH], FP8, name="qc")
+        qh = keep.tile([P, MT, CH], FP8, name="qh")
+        uT = [keep.tile([P, 2, N, 2], BF16, name="uT%d" % k) for k in range(NS)]
+        wgr = [keep.tile([P, NPASS * N * 4], BF16, name="wgr%d" % k, align_bytes=64) for k in range(NS)]
+        wc = [keep.tile([P, NPASS * N], U32, name="wc%d" % k, align_bytes=64) for k in range(NS)]
+        ws = [keep.tile([P, NPASS * N], U8, name="ws%d" % k, align_bytes=64) for k in range(NS)]
+
+        def copy_out(eng, out, in_):
+            if eng == "v":
+                nc.vector.tensor_copy(out=out, in_=in_)
+            else:
+                nc.scalar.copy(out=out, in_=in_)
+
+        def t_h(src, dst, eng):
+            pt = psT.tile([P, KT, P], BF16, name="pt", tag="T")
+            for kt in range(KT):
+                j, e = divmod(kt, 2)
+                nc.tensor.transpose(pt[:, kt, :], src[:, 256 * j + e : 256 * (j + 1) : 2], ident_b[:])
+            copy_out(eng, dst, pt[:])
+
+        def t_words(src, dst, eng):
+            words = src.bitcast(F32)
+            pw = psT.tile([P, NPASS, 2, P], F32, name="pw", tag="T")
+            for g in range(NPASS):
+                for u in range(2):
+                    nc.tensor.transpose(
+                        pw[:, g, u, :], words[:, 256 * g + u : 256 * (g + 1) : 2], ident_f[:]
+                    )
+            copy_out(eng, dst, pw[:].rearrange("p g u c -> p g c u"))
+
+        def word_view(t):
+            return t[:].bitcast(F32).rearrange("p (g c u) -> p g c u", g=NPASS, u=2)
+
+        def tu(k, eng):
+            pu = psT.tile([P, NB, 2, P], F32, name="pu", tag="T")
+            for b in range(NB):
+                words = u_in[k][b].bitcast(F32)
+                for j in range(2):
+                    nc.tensor.transpose(pu[:, b, j, :], words[:, j * P : (j + 1) * P], ident_f[:])
+            dst = uT[k][:].rearrange("p j c e -> p (j c e)").bitcast(F32).rearrange("p (j b c) -> p j b c", j=2, b=NB)
+            copy_out(eng, dst, pu[:].rearrange("p b j c -> p j b c"))
+
+        def tw(k, j, eng):
+            t_words(w_in[k][j], word_view(wgr[k])[:, :, j * P : (j + 1) * P, :], eng)
+
+        def quant(k):
+            nc.vector.quantize_mx(out=wc[k][:].bitcast(FP8X4), scales=ws[k][:], in_=wgr[k][:])
+
+        def mm_bias(k, out):
+            lo = 2 * CH + (k - NA) * N
+            nc.tensor.matmul(out=out, lhsT=ones[:], rhs=bias_row[:, lo : lo + N], start=True, stop=False)
+
+        def mm_p(k, out, m, kt):
+            nc.tensor.matmul(
+                out=out,
+                lhsT=hT[:, kt, m, :],
+                rhs=uT[k][:, kt // 2, :, kt % 2],
+                start=(kt == 0 and k < NA),
+                stop=(kt == KT - 1),
+            )
+
+        def mm_x(k, out, m, g):
+            zcols = slice((m * NPASS + g) * P, (m * NPASS + g + 1) * P)
+            wcols = slice(g * N, (g + 1) * N)
+            nc.tensor.matmul_mx(
+                out=out,
+                lhsT=zc[:, zcols].bitcast(FP8X4),
+                lhsT_scale=zs[:, zcols],
+                rhs=wc[k][:, wcols].bitcast(FP8X4),
+                rhs_scale=ws[k][:, wcols],
+                start=(g == 0),
+                stop=(g == NPASS - 1),
+            )
+
+        def absmax(j, lo, hi):
+            for m in range(MT):
+                nc.vector.tensor_reduce(
+                    out=pmx[:, j, m : m + 1], in_=c_sb[:, m, lo:hi], axis=AX.X, op=ALU.max, apply_absolute_value=True
+                )
+
+        def cast(eng, out, in_, m):
+            if eng == "v":
+                nc.vector.tensor_scalar(
+                    out=out, in0=in_, scalar1=rs[:, m : m + 1], scalar2=None, op0=ALU.mult, saturate=False
+                )
+            else:
+                nc.scalar.activation(
+                    out=out, in_=in_, func=ACT.Identity, scale=rs[:, m : m + 1], bias=zcol[:, 0:1], saturate=False
+                )
+
+        x_of = {}
+
+        with tc.manual_schedule():
+            t_h(h_in[0], hT[:, :, 0, :], "v")
+            t_h(h_in[1], hT[:, :, 1, :], "s")
+            tu(0, "s")
+            def bias_tile(j):
+                pbias = psT.tile([P, CH], F32, name="pbias", tag="T")
+                nc.tensor.matmul(
+                    out=pbias[:], lhsT=ones[:], rhs=bias_row[:, j * CH : (j + 1) * CH], start=True, stop=True
+                )
+                copy_out("s" if j == 0 else "v", bias_sb[:, j, :], pbias[:])
+
+            pt_first = psP.tile([P, MT * N], F32, name="pt_acc", tag="P")
+            bias_tile(0)
+            t_words(z_in[0], word_view(zgr[0]), "v")
+            bias_tile(1)
+            t_words(z_in[1], word_view(zgr[1]), "s")
+            mm_p(0, pt_first[:, 0:N], 0, 0)
+            mm_p(0, pt_first[:, 0:N], 0, 1)
+            tw(0, 0, "v")
+            mm_p(0, pt_first[:, 0:N], 0, 2)
+            mm_p(0, pt_first[:, 0:N], 0, 3)
+            tw(0, 1, "s")
+            for m in range(MT):
+                zcols = slice(m * NPASS * P, (m + 1) * NPASS * P)
+                nc.vector.quantize_mx(out=zc[:, zcols].bitcast(FP8X4), scales=zs[:, zcols], in_=zgr[m][:])
+            quant(0)
+            mm_p(0, pt_first[:, N : 2 * N], 1, 0)
+            mm_p(0, pt_first[:, N : 2 * N], 1, 1)
+            tw(1, 0, "s")
+            tw(1, 1, "s")
+            tu(1, "s")
+            quant(1)
+
+            for k in range(NS - 1):
+                pt_acc = pt_first if k == 0 else psP.tile([P, MT * N], F32, name="pt_acc", tag="P")
+                xt_acc = psX.tile([P, MT * N], F32, name="xt_acc", tag="X")
+                pb = ep.tile([P, MT, NB, P], F32, name="pb")
+                x = ep.tile([P, MT, NB, P], F32, name="x")
+                x_of[k] = x
+                prev = slice((k - 1) * P, k * P)
+                if k == 3:
+                    absmax(0, 0, 2 * P)
+                if k == 4:
+                    absmax(1, 2 * P, 3 * P)
+                if k >= 1:
+                    tw(k + 1, 0, "s")
+                    tw(k + 1, 1, "s")
+                    gi = ep.tile([P, MT, P], F32, name="gi")
+                    nc.scalar.activation(out=gi[:], in_=x_of[k - 1][:, :, 0, :], func=ACT.Sigmoid)
+                    gu = ep.tile([P, MT, P], F32, name="gu")
+                    nc.scalar.activation(out=gu[:], in_=x_of[k - 1][:, :, 1, :], func=ACT.Tanh)
+                    iu = ep.tile([P, MT, P], F32, name="iu")
+                if k >= 2:
+                    cols = slice((k - 2) * P, (k - 1) * P)
+                    nc.scalar.activation(out=tch[:, :, cols], in_=c_sb[:, :, cols], func=ACT.Tanh)
+                if k >= NA:
+                    mm_bias(k, pt_acc[:, 0:N])
+                if k >= 1:
+                    for kt in range(KT):
+                        mm_p(k, pt_acc[:, 0:N], 0, kt)
+                    if k < NA:
+                        tu(k + 1, "s")
+                    if k == NA - 1:
+                        tu(k + 2, "s")
+                    quant(k + 1)
+                if k == 4:
+                    nc.vector.tensor_tensor(out=mab[:], in0=pmx[:, 0, :], in1=pmx[:, 1, :], op=ALU.max)
+                if k >= 1:
+                    nc.vector.tensor_tensor(out=iu[:], in0=gi[:], in1=gu[:], op=ALU.mult)
+                if k < NA:
+                    for kt in range(2 if k == 0 else 0, KT - 1):
+                        mm_p(k, pt_acc[:, N : 2 * N], 1, kt)
+                    for m in range(MT):
+                        for g in range(NPASS):
+                            mm_x(k, xt_acc[:, m * N : (m + 1) * N], m, g)
+                    mm_p(k, pt_acc[:, N : 2 * N], 1, KT - 1)
+                    nc.vector.tensor_tensor(
+                        out=pb[:],
+                        in0=pt_acc[:].rearrange("p (m j c) -> p m j c", m=MT, j=NB),
+                        in1=bias_sb[:, :, k * P : (k + 1) * P].unsqueeze(1).to_broadcast([P, MT, NB, P]),
+                        op=ALU.add,
+                    )
+                    if k >= 1:
+                        nc.vector.tensor_tensor(out=c_sb[:, :, prev], in0=iu[:], in1=fc_sb[:, :, prev], op=ALU.add)
+                    nc.vector.tensor_tensor(
+                        out=x[:], in0=xt_acc[:].rearrange("p (m j c) -> p m j c", m=MT, j=NB), in1=pb[:], op=ALU.add
+                    )
+                else:
+                    mm_bias(k, pt_acc[:, N : 2 * N])
+                    for kt in range(KT):
+                        mm_p(k, pt_acc[:, N : 2 * N], 1, kt)
+                    nc.scalar.copy(out=pb[:], in_=pt_acc[:].rearrange("p (m j c) -> p m j c", m=MT, j=NB))
+                    for m in range(MT):
+                        for g in range(NPASS):
+                            mm_x(k, xt_acc[:, m * N : (m + 1) * N], m, g)
+                    nc.vector.tensor_scalar(out=sab[:], in0=mab[:], scalar1=1.0 / 448.0, scalar2=None, op0=ALU.mult)
+                    nc.vector.tensor_tensor(out=c_sb[:, :, prev], in0=iu[:], in1=fc_sb[:, :, prev], op=ALU.add)
+
+            k = NS - 1
+            p5 = []
+            x5 = []
+            for m in range(MT):
+                p5.append(psP.tile([P, N], F32, name="p5_%d" % m, tag="P"))
+                mm_bias(k, p5[m][:])
+                for kt in range(KT):
+                    mm_p(k, p5[m][:], m, kt)
+            for m in range(MT):
+                x5.append(psT.tile([P, N], F32, name="x5_%d" % m, tag="T"))
+                for g in range(NPASS):
+                    mm_x(k, x5[m][:], m, g)
+            x4 = x_of[NS - 2]
+            nc.vector.tensor_tensor(
+                out=x4[:], in0=xt_acc[:].rearrange("p (m j c) -> p m j c", m=MT, j=NB), in1=pb[:], op=ALU.add
+            )
+            pb5 = [ep.tile([P, N], F32, name="pb5_%d" % m, bufs=1) for m in range(MT)]
+            xs5 = [ep.tile([P, N], F32, name="xs5_%d" % m, bufs=1) for m in range(MT)]
+            go5 = [ep.tile([P, N], F32, name="go5_%d" % m, bufs=1) for m in range(MT)]
+            go4 = ep.tile([P, MT, N], F32, name="go4", bufs=1)
+            nc.scalar.copy(out=pb5[0][:], in_=p5[0][:])
+            nc.scalar.activation(out=tch[:, :, 3 * P : CH], in_=c_sb[:, :, 3 * P : CH], func=ACT.Tanh)
+            nc.scalar.copy(out=pb5[1][:], in_=p5[1][:])
+            nc.scalar.activation(out=go4[:], in_=x4[:].rearrange("p m j c -> p m (j c)"), func=ACT.Sigmoid)
+            absmax(2, 3 * P, CH)
+            nc.sync.dma_start(out=out0v[:, :, CH : 2 * CH], in_=c_sb[:])
+            nc.vector.tensor_tensor(out=xs5[0][:], in0=x5[0][:], in1=pb5[0][:], op=ALU.add)
+            nc.vector.scalar_tensor_tensor(
+                out=sc[:], in0=pmx[:, 2, :], scalar=1.0 / 448.0, in1=sab[:], op0=ALU.mult, op1=ALU.max
+            )
+            nc.vector.tensor_tensor(out=xs5[1][:], in0=x5[1][:], in1=pb5[1][:], op=ALU.add)
+            nc.vector.reciprocal(out=rs[:], in_=sc[:])
+            for m in range(MT):
+                nc.scalar.activation(out=go5[m][:], in_=xs5[m][:], func=ACT.Sigmoid)
+            nc.vector.tensor_tensor(out=h_sb[:, :, 0:N], in0=go4[:], in1=tch[:, :, 0:N], op=ALU.mult)
+            nc.sync.dma_start(out=out0v[:, :, 0:N], in_=h_sb[:, :, 0:N])
+            for m in range(MT):
+                nc.vector.tensor_tensor(out=h_sb[:, m, N:CH], in0=go5[m][:], in1=tch[:, m, N:CH], op=ALU.mult)
+            nc.sync.dma_start(out=out0v[:, :, N:CH], in_=h_sb[:, :, N:CH])
+            for m in range(MT):
+                cast("s", qc[:, m, :], c_sb[:, m, :], m)
+            nc.sync.dma_start(out=out1v[:, :, CH : 2 * CH], in_=qc[:].bitcast(U8))
+            cast("s", qh[:, 0, 0:N], h_sb[:, 0, 0:N], 0)
+            for m in range(MT):
+                cast("v", qh[:, m, N:CH], h_sb[:, m, N:CH], m)
+            cast("v", qh[:, 1, 0:N], h_sb[:, 1, 0:N], 1)
+            nc.sync.dma_start(out=out1v[:, :, 0:CH], in_=qh[:].bitcast(U8))

@@ -24,6 +24,7 @@ NB = 2
 N = NB * P
 NA = 4
 NS = 6
+LAST = NS - 1
 
 
 def tile_treelstm_pb_kernel(
@@ -39,25 +40,21 @@ def tile_treelstm_pb_kernel(
         keep = ctx.enter_context(tc.tile_pool(name="keep", bufs=1))
         ep = ctx.enter_context(tc.tile_pool(name="ep", bufs=3))
         psT = ctx.enter_context(tc.psum_pool(name="psT", bufs=4))
-        psP = ctx.enter_context(tc.psum_pool(name="psP", bufs=2))
-        psX = ctx.enter_context(tc.psum_pool(name="psX", bufs=2))
+        psP = ctx.enter_context(tc.psum_pool(name="psP", bufs=3))
+        psX = ctx.enter_context(tc.psum_pool(name="psX", bufs=1))
 
-        bias_row = const.tile([P, 3 * CH], BF16, name="bias_row")
-        nc.vector.memset(bias_row[:], 0.0)
+        bias_rows = const.tile([P, P], BF16, name="bias_rows")
+        nc.vector.memset(bias_rows[:], 0.0)
         for j, b in enumerate((b_i, b_u, b_o)):
-            nc.scalar.dma_start(
-                out=bias_row[0:1, j * CH : (j + 1) * CH], in_=b.rearrange("(o c) -> o c", o=1)
-            )
-        ones = const.tile([P, P], BF16, name="ones")
-        nc.vector.memset(ones[:], 1.0)
+            nc.scalar.dma_start(out=bias_rows[j * KT : (j + 1) * KT, :], in_=b.rearrange("(t c) -> t c", c=P))
         zcol = const.tile([P, 1], F32, name="zcol")
         nc.vector.memset(zcol[:], 0.0)
         warm = const.tile([P, 1], F32, name="warm")
         nc.scalar.activation(out=warm[:], in_=zcol[:], func=ACT.Sigmoid)
-        ident_b = const.tile([P, P], BF16, name="ident_b")
-        make_identity(nc, ident_b[:])
         ident_f = const.tile([P, P], F32, name="ident_f")
         make_identity(nc, ident_f[:])
+        ident_b = const.tile([P, P], BF16, name="ident_b")
+        make_identity(nc, ident_b[:])
 
         def load_rows(dram, r0, nrt, width, name):
             t = inp.tile([P, nrt, width], BF16, name=name)
@@ -68,14 +65,18 @@ def tile_treelstm_pb_kernel(
 
         u_in = {}
         w_in = {}
+
+        def load_u(k):
+            u_in[k] = load_rows(U_i, k, 1, CH, "Ui%d" % k) + load_rows(U_u, k, 1, CH, "Uu%d" % k)
+
         h_in = load_rows(h_tilde, 0, 1, CH, "h_in0") + load_rows(h_tilde, 1, 1, CH, "h_in1")
-        u_in[0] = load_rows(U_i, 0, 1, CH, "Ui0") + load_rows(U_u, 0, 1, CH, "Uu0")
+        load_u(0)
         z_in = load_rows(z0, 0, 1, SIZE, "z_in0") + load_rows(z0, 1, 1, SIZE, "z_in1")
         fc_sb = inp.tile([P, MT, CH], BF16, name="fc_sb")
         for k in range(NA):
             w_in[k] = load_rows(W_i, k, 1, SIZE, "Wi%d" % k) + load_rows(W_u, k, 1, SIZE, "Wu%d" % k)
             if k >= 1:
-                u_in[k] = load_rows(U_i, k, 1, CH, "Ui%d" % k) + load_rows(U_u, k, 1, CH, "Uu%d" % k)
+                load_u(k)
             if k == 2:
                 nc.sync.dma_start(out=fc_sb[:], in_=fc_sum.rearrange("(m p) c -> p m c", p=P))
         w_in[NA] = load_rows(W_o, 0, NB, SIZE, "Wo0")
@@ -84,17 +85,16 @@ def tile_treelstm_pb_kernel(
         u_in[NA + 1] = u_o[NB : 2 * NB]
         w_in[NA + 1] = load_rows(W_o, NB, NB, SIZE, "Wo1")
 
-        hT = keep.tile([P, KT, MT, P], BF16, name="hT")
-        zgr = [keep.tile([P, NPASS * P * 4], BF16, name="zgr%d" % m, align_bytes=64) for m in range(MT)]
-        zc = keep.tile([P, MT * NPASS * P], U32, name="zc", align_bytes=64)
-        zs = keep.tile([P, MT * NPASS * P], U8, name="zs", align_bytes=64)
-        bias_sb = keep.tile([P, 2, CH], F32, name="bias_sb")
+        hT = keep.tile([P, 2, MT, P, 2], BF16, name="hT")
+        zgr = keep.tile([P, NPASS * MT * P * 4], BF16, name="zgr", align_bytes=64)
+        zc = keep.tile([P, NPASS * MT * P], U32, name="zc", align_bytes=64)
+        zs = keep.tile([P, NPASS * MT * P], U8, name="zs", align_bytes=64)
+        bias_sb = keep.tile([P, KT, 3], F32, name="bias_sb")
         c_sb = keep.tile([P, MT, CH], F32, name="c_sb")
         tch = keep.tile([P, MT, CH], F32, name="tch")
         h_sb = keep.tile([P, MT, CH], F32, name="h_sb")
-        pmx = keep.tile([P, 3, MT], F32, name="pmx")
+        pmx = keep.tile([P, 2, MT], F32, name="pmx")
         mab = keep.tile([P, MT], F32, name="mab")
-        sab = keep.tile([P, MT], F32, name="sab")
         sc = keep.tile([P, MT], F32, name="sc")
         rs = keep.tile([P, MT], F32, name="rs")
         qc = keep.tile([P, MT, CH], FP8, name="qc")
@@ -110,12 +110,13 @@ def tile_treelstm_pb_kernel(
             else:
                 nc.scalar.copy(out=out, in_=in_)
 
-        def t_h(src, dst, eng):
-            pt = psT.tile([P, KT, P], BF16, name="pt", tag="T")
-            for kt in range(KT):
-                j, e = divmod(kt, 2)
-                nc.tensor.transpose(pt[:, kt, :], src[:, 256 * j + e : 256 * (j + 1) : 2], ident_b[:])
-            copy_out(eng, dst, pt[:])
+        def t_h(eng):
+            pt = psT.tile([P, 2, MT, P], F32, name="pt", tag="T")
+            for m in range(MT):
+                words = h_in[m].bitcast(F32)
+                for j in range(2):
+                    nc.tensor.transpose(pt[:, j, m, :], words[:, j * P : (j + 1) * P], ident_f[:])
+            copy_out(eng, hT[:].rearrange("p j m r e -> p (j m r e)").bitcast(F32), pt[:].rearrange("p j m r -> p (j m r)"))
 
         def t_words(src, dst, eng):
             words = src.bitcast(F32)
@@ -130,6 +131,12 @@ def tile_treelstm_pb_kernel(
         def word_view(t):
             return t[:].bitcast(F32).rearrange("p (g c u) -> p g c u", g=NPASS, u=2)
 
+        def tz(m, eng):
+            t_words(z_in[m], word_view(zgr)[:, :, m * P : (m + 1) * P, :], eng)
+
+        def tw(k, j, eng):
+            t_words(w_in[k][j], word_view(wgr[k])[:, :, j * P : (j + 1) * P, :], eng)
+
         def tu(k, eng):
             pu = psT.tile([P, NB, 2, P], F32, name="pu", tag="T")
             for b in range(NB):
@@ -139,37 +146,54 @@ def tile_treelstm_pb_kernel(
             dst = uT[k][:].rearrange("p j c e -> p (j c e)").bitcast(F32).rearrange("p (j b c) -> p j b c", j=2, b=NB)
             copy_out(eng, dst, pu[:].rearrange("p b j c -> p j b c"))
 
-        def tw(k, j, eng):
-            t_words(w_in[k][j], word_view(wgr[k])[:, :, j * P : (j + 1) * P, :], eng)
-
         def quant(k):
             nc.vector.quantize_mx(out=wc[k][:].bitcast(FP8X4), scales=ws[k][:], in_=wgr[k][:])
 
-        def mm_bias(k, out):
-            lo = 2 * CH + (k - NA) * N
-            nc.tensor.matmul(out=out, lhsT=ones[:], rhs=bias_row[:, lo : lo + N], start=True, stop=False)
-
-        def mm_p(k, out, m, kt):
+        def mm_p(k, out, m, kt, start):
             nc.tensor.matmul(
-                out=out,
-                lhsT=hT[:, kt, m, :],
-                rhs=uT[k][:, kt // 2, :, kt % 2],
-                start=(kt == 0 and k < NA),
-                stop=(kt == KT - 1),
+                out=out, lhsT=hT[:, kt // 2, m, :, kt % 2], rhs=uT[k][:, kt // 2, :, kt % 2], start=start, stop=False
             )
 
-        def mm_x(k, out, m, g):
-            zcols = slice((m * NPASS + g) * P, (m * NPASS + g + 1) * P)
-            wcols = slice(g * N, (g + 1) * N)
-            nc.tensor.matmul_mx(
-                out=out,
-                lhsT=zc[:, zcols].bitcast(FP8X4),
-                lhsT_scale=zs[:, zcols],
-                rhs=wc[k][:, wcols].bitcast(FP8X4),
-                rhs_scale=ws[k][:, wcols],
-                start=(g == 0),
-                stop=(g == NPASS - 1),
-            )
+        def mm_x(k, xt):
+            for j in range(NB):
+                for g in range(NPASS):
+                    zcols = slice(g * MT * P, (g + 1) * MT * P)
+                    wcols = slice(g * N + j * P, g * N + (j + 1) * P)
+                    nc.tensor.matmul_mx(
+                        out=xt[:, j, :],
+                        lhsT=wc[k][:, wcols].bitcast(FP8X4),
+                        lhsT_scale=ws[k][:, wcols],
+                        rhs=zc[:, zcols].bitcast(FP8X4),
+                        rhs_scale=zs[:, zcols],
+                        start=(g == 0),
+                        stop=(g == NPASS - 1),
+                    )
+
+        def x_out(k, xt, eng):
+            xs = ep.tile([P, NB, MT * P], F32, name="xs")
+            if k < NA:
+                b = bias_sb[:, k, 0:NB]
+            else:
+                b = bias_sb[:, (k - NA) * NB : (k - NA + 1) * NB, 2]
+            if eng == "v":
+                nc.vector.tensor_tensor(
+                    out=xs[:], in0=xt[:], in1=b.unsqueeze(2).to_broadcast([P, NB, MT * P]), op=ALU.add
+                )
+            else:
+                for j in range(NB):
+                    nc.scalar.activation(out=xs[:, j, :], in_=xt[:, j, :], func=ACT.Identity, bias=b[:, j : j + 1])
+            return xs
+
+        def t_add(out, xs, m, stop):
+            for j in range(NB):
+                nc.tensor.matmul(
+                    out=out[:, j * P : (j + 1) * P],
+                    lhsT=xs[:, j, m * P : (m + 1) * P],
+                    rhs=ident_f[:],
+                    start=False,
+                    stop=(stop and j == NB - 1),
+                    is_transpose=True,
+                )
 
         def absmax(j, lo, hi):
             for m in range(MT):
@@ -187,150 +211,102 @@ def tile_treelstm_pb_kernel(
                     out=out, in_=in_, func=ACT.Identity, scale=rs[:, m : m + 1], bias=zcol[:, 0:1], saturate=False
                 )
 
-        x_of = {}
+        def plain(k, out, m, start):
+            for kt in range(KT):
+                mm_p(k, out, m, kt, start and kt == 0)
+
+        p_of = {}
+        xs_of = {}
+
+        def new_acc(k):
+            p_of[k] = psP.tile([P, MT, N], F32, name="acc", tag="P")
+
+        def x_tile():
+            return psX.tile([P, NB, MT * P], F32, name="xt", tag="X")
+
+        def add_x(k):
+            for m in range(MT):
+                t_add(p_of[k][:, m, :], xs_of[k], m, m == MT - 1)
 
         with tc.manual_schedule():
-            t_h(h_in[0], hT[:, :, 0, :], "v")
-            t_h(h_in[1], hT[:, :, 1, :], "s")
+            t_h("v")
             tu(0, "s")
-            def bias_tile(j):
-                pbias = psT.tile([P, CH], F32, name="pbias", tag="T")
-                nc.tensor.matmul(
-                    out=pbias[:], lhsT=ones[:], rhs=bias_row[:, j * CH : (j + 1) * CH], start=True, stop=True
-                )
-                copy_out("s" if j == 0 else "v", bias_sb[:, j, :], pbias[:])
-
-            pt_first = psP.tile([P, MT * N], F32, name="pt_acc", tag="P")
-            bias_tile(0)
-            t_words(z_in[0], word_view(zgr[0]), "v")
-            bias_tile(1)
-            t_words(z_in[1], word_view(zgr[1]), "s")
-            mm_p(0, pt_first[:, 0:N], 0, 0)
-            mm_p(0, pt_first[:, 0:N], 0, 1)
+            pbias = psT.tile([P, P], BF16, name="pbias", tag="T")
+            nc.tensor.transpose(pbias[:], bias_rows[:], ident_b[:])
+            nc.scalar.copy(out=bias_sb[:], in_=pbias[:, 0 : 3 * KT].rearrange("p (g t) -> p t g", g=3))
+            tz(0, "v")
+            tz(1, "s")
+            new_acc(0)
+            plain(0, p_of[0][:, 0, :], 0, True)
             tw(0, 0, "v")
-            mm_p(0, pt_first[:, 0:N], 0, 2)
-            mm_p(0, pt_first[:, 0:N], 0, 3)
             tw(0, 1, "s")
-            for m in range(MT):
-                zcols = slice(m * NPASS * P, (m + 1) * NPASS * P)
-                nc.vector.quantize_mx(out=zc[:, zcols].bitcast(FP8X4), scales=zs[:, zcols], in_=zgr[m][:])
+            nc.vector.quantize_mx(out=zc[:].bitcast(FP8X4), scales=zs[:], in_=zgr[:])
+            plain(0, p_of[0][:, 1, :], 1, False)
             quant(0)
-            mm_p(0, pt_first[:, N : 2 * N], 1, 0)
-            mm_p(0, pt_first[:, N : 2 * N], 1, 1)
-            tw(1, 0, "s")
-            tw(1, 1, "s")
-            tu(1, "s")
-            quant(1)
 
             for k in range(NS - 1):
-                pt_acc = pt_first if k == 0 else psP.tile([P, MT * N], F32, name="pt_acc", tag="P")
-                xt_acc = psX.tile([P, MT * N], F32, name="xt_acc", tag="X")
-                pb = ep.tile([P, MT, NB, P], F32, name="pb")
-                x = ep.tile([P, MT, NB, P], F32, name="x")
-                x_of[k] = x
                 prev = slice((k - 1) * P, k * P)
-                if k == 3:
-                    absmax(0, 0, 2 * P)
-                if k == 4:
-                    absmax(1, 2 * P, 3 * P)
+                tw(k + 1, 0, "s")
+                tw(k + 1, 1, "s")
+                quant(k + 1)
                 if k >= 1:
-                    tw(k + 1, 0, "s")
-                    tw(k + 1, 1, "s")
+                    new_acc(k)
+                    add_x(k - 1)
                     gi = ep.tile([P, MT, P], F32, name="gi")
-                    nc.scalar.activation(out=gi[:], in_=x_of[k - 1][:, :, 0, :], func=ACT.Sigmoid)
+                    nc.scalar.activation(out=gi[:], in_=p_of[k - 1][:, :, 0:P], func=ACT.Sigmoid)
                     gu = ep.tile([P, MT, P], F32, name="gu")
-                    nc.scalar.activation(out=gu[:], in_=x_of[k - 1][:, :, 1, :], func=ACT.Tanh)
+                    nc.scalar.activation(out=gu[:], in_=p_of[k - 1][:, :, P:N], func=ACT.Tanh)
+                    plain(k, p_of[k][:, 0, :], 0, True)
                     iu = ep.tile([P, MT, P], F32, name="iu")
+                xt = x_tile()
+                mm_x(k, xt)
+                if k == NA:
+                    nc.vector.tensor_tensor(out=iu[:], in0=gi[:], in1=gu[:], op=ALU.mult)
+                xs_of[k] = x_out(k, xt, "v")
+                if 1 <= k < NA:
+                    nc.vector.tensor_tensor(out=iu[:], in0=gi[:], in1=gu[:], op=ALU.mult)
+                if k >= 1:
+                    plain(k, p_of[k][:, 1, :], 1, False)
                 if k >= 2:
                     cols = slice((k - 2) * P, (k - 1) * P)
                     nc.scalar.activation(out=tch[:, :, cols], in_=c_sb[:, :, cols], func=ACT.Tanh)
-                if k >= NA:
-                    mm_bias(k, pt_acc[:, 0:N])
-                if k >= 1:
-                    for kt in range(KT):
-                        mm_p(k, pt_acc[:, 0:N], 0, kt)
-                    if k < NA:
-                        tu(k + 1, "s")
-                    if k == NA - 1:
-                        tu(k + 2, "s")
-                    quant(k + 1)
-                if k == 4:
-                    nc.vector.tensor_tensor(out=mab[:], in0=pmx[:, 0, :], in1=pmx[:, 1, :], op=ALU.max)
-                if k >= 1:
-                    nc.vector.tensor_tensor(out=iu[:], in0=gi[:], in1=gu[:], op=ALU.mult)
                 if k < NA:
-                    for kt in range(2 if k == 0 else 0, KT - 1):
-                        mm_p(k, pt_acc[:, N : 2 * N], 1, kt)
-                    for m in range(MT):
-                        for g in range(NPASS):
-                            mm_x(k, xt_acc[:, m * N : (m + 1) * N], m, g)
-                    mm_p(k, pt_acc[:, N : 2 * N], 1, KT - 1)
-                    nc.vector.tensor_tensor(
-                        out=pb[:],
-                        in0=pt_acc[:].rearrange("p (m j c) -> p m j c", m=MT, j=NB),
-                        in1=bias_sb[:, :, k * P : (k + 1) * P].unsqueeze(1).to_broadcast([P, MT, NB, P]),
-                        op=ALU.add,
-                    )
-                    if k >= 1:
-                        nc.vector.tensor_tensor(out=c_sb[:, :, prev], in0=iu[:], in1=fc_sb[:, :, prev], op=ALU.add)
-                    nc.vector.tensor_tensor(
-                        out=x[:], in0=xt_acc[:].rearrange("p (m j c) -> p m j c", m=MT, j=NB), in1=pb[:], op=ALU.add
-                    )
-                else:
-                    mm_bias(k, pt_acc[:, N : 2 * N])
-                    for kt in range(KT):
-                        mm_p(k, pt_acc[:, N : 2 * N], 1, kt)
-                    nc.scalar.copy(out=pb[:], in_=pt_acc[:].rearrange("p (m j c) -> p m j c", m=MT, j=NB))
-                    for m in range(MT):
-                        for g in range(NPASS):
-                            mm_x(k, xt_acc[:, m * N : (m + 1) * N], m, g)
-                    nc.vector.tensor_scalar(out=sab[:], in0=mab[:], scalar1=1.0 / 448.0, scalar2=None, op0=ALU.mult)
+                    tu(k + 1, "v")
+                if k == NA - 1:
+                    tu(k + 2, "v")
+                if k == NA - 1:
+                    absmax(0, 0, 2 * P)
+                if k >= 1:
                     nc.vector.tensor_tensor(out=c_sb[:, :, prev], in0=iu[:], in1=fc_sb[:, :, prev], op=ALU.add)
 
-            k = NS - 1
-            p5 = []
-            x5 = []
-            for m in range(MT):
-                p5.append(psP.tile([P, N], F32, name="p5_%d" % m, tag="P"))
-                mm_bias(k, p5[m][:])
-                for kt in range(KT):
-                    mm_p(k, p5[m][:], m, kt)
-            for m in range(MT):
-                x5.append(psT.tile([P, N], F32, name="x5_%d" % m, tag="T"))
-                for g in range(NPASS):
-                    mm_x(k, x5[m][:], m, g)
-            x4 = x_of[NS - 2]
-            nc.vector.tensor_tensor(
-                out=x4[:], in0=xt_acc[:].rearrange("p (m j c) -> p m j c", m=MT, j=NB), in1=pb[:], op=ALU.add
-            )
-            pb5 = [ep.tile([P, N], F32, name="pb5_%d" % m, bufs=1) for m in range(MT)]
-            xs5 = [ep.tile([P, N], F32, name="xs5_%d" % m, bufs=1) for m in range(MT)]
-            go5 = [ep.tile([P, N], F32, name="go5_%d" % m, bufs=1) for m in range(MT)]
-            go4 = ep.tile([P, MT, N], F32, name="go4", bufs=1)
-            nc.scalar.copy(out=pb5[0][:], in_=p5[0][:])
-            nc.scalar.activation(out=tch[:, :, 3 * P : CH], in_=c_sb[:, :, 3 * P : CH], func=ACT.Tanh)
-            nc.scalar.copy(out=pb5[1][:], in_=p5[1][:])
-            nc.scalar.activation(out=go4[:], in_=x4[:].rearrange("p m j c -> p m (j c)"), func=ACT.Sigmoid)
-            absmax(2, 3 * P, CH)
             nc.sync.dma_start(out=out0v[:, :, CH : 2 * CH], in_=c_sb[:])
-            nc.vector.tensor_tensor(out=xs5[0][:], in0=x5[0][:], in1=pb5[0][:], op=ALU.add)
-            nc.vector.scalar_tensor_tensor(
-                out=sc[:], in0=pmx[:, 2, :], scalar=1.0 / 448.0, in1=sab[:], op0=ALU.mult, op1=ALU.max
-            )
-            nc.vector.tensor_tensor(out=xs5[1][:], in0=x5[1][:], in1=pb5[1][:], op=ALU.add)
-            nc.vector.reciprocal(out=rs[:], in_=sc[:])
+            p5 = [psP.tile([P, N], F32, name="p5_0", tag="P"), psT.tile([P, N], F32, name="p5_1", tag="T")]
+            xt = x_tile()
+            mm_x(LAST, xt)
+            xs_of[LAST] = x_out(LAST, xt, "s")
+            plain(LAST, p5[0][:], 0, True)
+            absmax(1, 2 * P, CH)
+            add_x(4)
+            nc.vector.tensor_tensor(out=mab[:], in0=pmx[:, 0, :], in1=pmx[:, 1, :], op=ALU.max)
+            go4 = ep.tile([P, MT, N], F32, name="go4", bufs=1)
+            nc.scalar.activation(out=tch[:, :, 3 * P : CH], in_=c_sb[:, :, 3 * P : CH], func=ACT.Tanh)
+            nc.scalar.activation(out=go4[:], in_=p_of[4][:], func=ACT.Sigmoid)
+            plain(LAST, p5[1][:], 1, True)
             for m in range(MT):
-                nc.scalar.activation(out=go5[m][:], in_=xs5[m][:], func=ACT.Sigmoid)
+                t_add(p5[m][:], xs_of[LAST], m, True)
+            nc.vector.tensor_scalar(out=sc[:], in0=mab[:], scalar1=1.0 / 448.0, scalar2=None, op0=ALU.mult)
             nc.vector.tensor_tensor(out=h_sb[:, :, 0:N], in0=go4[:], in1=tch[:, :, 0:N], op=ALU.mult)
             nc.sync.dma_start(out=out0v[:, :, 0:N], in_=h_sb[:, :, 0:N])
+            go5 = [ep.tile([P, N], F32, name="go5_%d" % m, bufs=1) for m in range(MT)]
+            for m in range(MT):
+                nc.scalar.activation(out=go5[m][:], in_=p5[m][:], func=ACT.Sigmoid)
+            nc.vector.reciprocal(out=rs[:], in_=sc[:])
             for m in range(MT):
                 nc.vector.tensor_tensor(out=h_sb[:, m, N:CH], in0=go5[m][:], in1=tch[:, m, N:CH], op=ALU.mult)
             nc.sync.dma_start(out=out0v[:, :, N:CH], in_=h_sb[:, :, N:CH])
             for m in range(MT):
                 cast("s", qc[:, m, :], c_sb[:, m, :], m)
             nc.sync.dma_start(out=out1v[:, :, CH : 2 * CH], in_=qc[:].bitcast(U8))
-            cast("s", qh[:, 0, 0:N], h_sb[:, 0, 0:N], 0)
             for m in range(MT):
-                cast("v", qh[:, m, N:CH], h_sb[:, m, N:CH], m)
-            cast("v", qh[:, 1, 0:N], h_sb[:, 1, 0:N], 1)
+                cast("v", qh[:, m, :], h_sb[:, m, :], m)
             nc.sync.dma_start(out=out1v[:, :, 0:CH], in_=qh[:].bitcast(U8))

@@ -25,6 +25,7 @@ N = NB * P
 NA = 4
 NS = 6
 LAST = NS - 1
+ORDERED = 3
 
 
 def tile_treelstm_pb_kernel(
@@ -45,8 +46,6 @@ def tile_treelstm_pb_kernel(
 
         bias_rows = const.tile([P, P], BF16, name="bias_rows")
         nc.vector.memset(bias_rows[:], 0.0)
-        for j, b in enumerate((b_i, b_u, b_o)):
-            nc.scalar.dma_start(out=bias_rows[j * KT : (j + 1) * KT, :], in_=b.rearrange("(t c) -> t c", c=P))
         zcol = const.tile([P, 1], F32, name="zcol")
         nc.vector.memset(zcol[:], 0.0)
         warm = const.tile([P, 1], F32, name="warm")
@@ -66,26 +65,40 @@ def tile_treelstm_pb_kernel(
         u_in = {}
         w_in = {}
 
+        def load_w(k):
+            t = inp.tile([P, NB, SIZE], BF16, name="W%d" % k)
+            if k < NA:
+                for j, W in enumerate((W_i, W_u)):
+                    nc.sync.dma_start(out=t[:, j, :], in_=W[k * P : (k + 1) * P, :])
+            else:
+                r0 = (k - NA) * N
+                nc.sync.dma_start(out=t[:], in_=W_o[r0 : r0 + N, :].rearrange("(t p) k -> p t k", p=P))
+            w_in[k] = t
+
         def load_u(k):
             u_in[k] = load_rows(U_i, k, 1, CH, "Ui%d" % k) + load_rows(U_u, k, 1, CH, "Uu%d" % k)
 
         h_in = load_rows(h_tilde, 0, 1, CH, "h_in0") + load_rows(h_tilde, 1, 1, CH, "h_in1")
         load_u(0)
+        load_u(1)
         z_in = load_rows(z0, 0, 1, SIZE, "z_in0") + load_rows(z0, 1, 1, SIZE, "z_in1")
+        load_w(0)
+        for j, b in enumerate((b_i, b_u, b_o)):
+            nc.sync.dma_start(out=bias_rows[j * KT : (j + 1) * KT, :], in_=b.rearrange("(t c) -> t c", c=P))
+        load_w(1)
+        load_u(2)
+        load_w(2)
         fc_sb = inp.tile([P, MT, CH], BF16, name="fc_sb")
-        for k in range(NA):
-            w_in[k] = load_rows(W_i, k, 1, SIZE, "Wi%d" % k) + load_rows(W_u, k, 1, SIZE, "Wu%d" % k)
-            if k >= 1:
-                load_u(k)
-            if k == 2:
-                nc.sync.dma_start(out=fc_sb[:], in_=fc_sum.rearrange("(m p) c -> p m c", p=P))
-        w_in[NA] = load_rows(W_o, 0, NB, SIZE, "Wo0")
+        nc.sync.dma_start(out=fc_sb[:], in_=fc_sum.rearrange("(m p) c -> p m c", p=P))
+        load_u(3)
+        load_w(3)
         u_o = load_rows(U_o, 0, 2 * NB, CH, "Uo")
         u_in[NA] = u_o[0:NB]
         u_in[NA + 1] = u_o[NB : 2 * NB]
-        w_in[NA + 1] = load_rows(W_o, NB, NB, SIZE, "Wo1")
+        load_w(NA)
+        load_w(NA + 1)
 
-        hT = keep.tile([P, 2, MT, P, 2], BF16, name="hT")
+        hT = keep.tile([P, MT, 2, P, 2], BF16, name="hT")
         zgr = keep.tile([P, NPASS * MT * P * 4], BF16, name="zgr", align_bytes=64)
         zc = keep.tile([P, NPASS * MT * P], U32, name="zc", align_bytes=64)
         zs = keep.tile([P, NPASS * MT * P], U8, name="zs", align_bytes=64)
@@ -93,13 +106,15 @@ def tile_treelstm_pb_kernel(
         c_sb = keep.tile([P, MT, CH], F32, name="c_sb")
         tch = keep.tile([P, MT, CH], F32, name="tch")
         h_sb = keep.tile([P, MT, CH], F32, name="h_sb")
-        pmx = keep.tile([P, 2, MT], F32, name="pmx")
+        pmx = keep.tile([P, 3, MT], F32, name="pmx")
         mab = keep.tile([P, MT], F32, name="mab")
+        sab = keep.tile([P, MT], F32, name="sab")
         sc = keep.tile([P, MT], F32, name="sc")
         rs = keep.tile([P, MT], F32, name="rs")
         qc = keep.tile([P, MT, CH], FP8, name="qc")
         qh = keep.tile([P, MT, CH], FP8, name="qh")
         uT = [keep.tile([P, 2, N, 2], BF16, name="uT%d" % k) for k in range(NS)]
+        wo = {k: keep.tile([P, NB, NPASS, 2, P], F32, name="wo%d" % k) for k in range(ORDERED, NS)}
         wgr = [keep.tile([P, NPASS * N * 4], BF16, name="wgr%d" % k, align_bytes=64) for k in range(NS)]
         wc = [keep.tile([P, NPASS * N], U32, name="wc%d" % k, align_bytes=64) for k in range(NS)]
         ws = [keep.tile([P, NPASS * N], U8, name="ws%d" % k, align_bytes=64) for k in range(NS)]
@@ -110,13 +125,12 @@ def tile_treelstm_pb_kernel(
             else:
                 nc.scalar.copy(out=out, in_=in_)
 
-        def t_h(eng):
-            pt = psT.tile([P, 2, MT, P], F32, name="pt", tag="T")
-            for m in range(MT):
-                words = h_in[m].bitcast(F32)
-                for j in range(2):
-                    nc.tensor.transpose(pt[:, j, m, :], words[:, j * P : (j + 1) * P], ident_f[:])
-            copy_out(eng, hT[:].rearrange("p j m r e -> p (j m r e)").bitcast(F32), pt[:].rearrange("p j m r -> p (j m r)"))
+        def t_h(m, eng):
+            pt = psT.tile([P, 2, P], F32, name="pt", tag="T")
+            words = h_in[m].bitcast(F32)
+            for j in range(2):
+                nc.tensor.transpose(pt[:, j, :], words[:, j * P : (j + 1) * P], ident_f[:])
+            copy_out(eng, hT[:, m].rearrange("p j r e -> p (j r e)").bitcast(F32), pt[:].rearrange("p j r -> p (j r)"))
 
         def t_words(src, dst, eng):
             words = src.bitcast(F32)
@@ -134,8 +148,22 @@ def tile_treelstm_pb_kernel(
         def tz(m, eng):
             t_words(z_in[m], word_view(zgr)[:, :, m * P : (m + 1) * P, :], eng)
 
+        def order_words(k):
+            nc.vector.tensor_copy(
+                out=wo[k][:].rearrange("p j g u q -> p (j g) u q"),
+                in_=w_in[k][:].bitcast(F32).rearrange("p j (g q u) -> p (j g) u q", g=NPASS, u=2),
+            )
+
         def tw(k, j, eng):
-            t_words(w_in[k][j], word_view(wgr[k])[:, :, j * P : (j + 1) * P, :], eng)
+            dst = word_view(wgr[k])[:, :, j * P : (j + 1) * P, :]
+            if k < ORDERED:
+                t_words(w_in[k][:, j, :], dst, eng)
+            else:
+                pw = psT.tile([P, NPASS, 2, P], F32, name="pw", tag="T")
+                for g in range(NPASS):
+                    for u in range(2):
+                        nc.tensor.transpose(pw[:, g, u, :], wo[k][:, j, g, u, :], ident_f[:])
+                copy_out(eng, dst, pw[:].rearrange("p g u c -> p g c u"))
 
         def tu(k, eng):
             pu = psT.tile([P, NB, 2, P], F32, name="pu", tag="T")
@@ -151,7 +179,7 @@ def tile_treelstm_pb_kernel(
 
         def mm_p(k, out, m, kt, start):
             nc.tensor.matmul(
-                out=out, lhsT=hT[:, kt // 2, m, :, kt % 2], rhs=uT[k][:, kt // 2, :, kt % 2], start=start, stop=False
+                out=out, lhsT=hT[:, m, kt // 2, :, kt % 2], rhs=uT[k][:, kt // 2, :, kt % 2], start=start, stop=False
             )
 
         def mm_x(k, xt):
@@ -169,20 +197,23 @@ def tile_treelstm_pb_kernel(
                         stop=(g == NPASS - 1),
                     )
 
-        def x_out(k, xt, eng):
-            xs = ep.tile([P, NB, MT * P], F32, name="xs")
-            if k < NA:
-                b = bias_sb[:, k, 0:NB]
-            else:
-                b = bias_sb[:, (k - NA) * NB : (k - NA + 1) * NB, 2]
+        def x_bias(k):
+            return bias_sb[:, k, 0:NB] if k < NA else bias_sb[:, (k - NA) * NB : (k - NA + 1) * NB, 2]
+
+        def x_out(k, xt):
+            xs_of[k] = ep.tile([P, NB, MT * P], F32, name="xs")
+            nc.vector.tensor_tensor(
+                out=xs_of[k][:], in0=xt[:], in1=x_bias(k).unsqueeze(2).to_broadcast([P, NB, MT * P]), op=ALU.add
+            )
+
+        def x_out_half(k, xt, j, eng):
+            b = x_bias(k)[:, j : j + 1]
             if eng == "v":
-                nc.vector.tensor_tensor(
-                    out=xs[:], in0=xt[:], in1=b.unsqueeze(2).to_broadcast([P, NB, MT * P]), op=ALU.add
+                nc.vector.tensor_scalar(
+                    out=xs_of[k][:, j, :], in0=xt[:, j, :], scalar1=b, scalar2=None, op0=ALU.add
                 )
             else:
-                for j in range(NB):
-                    nc.scalar.activation(out=xs[:, j, :], in_=xt[:, j, :], func=ACT.Identity, bias=b[:, j : j + 1])
-            return xs
+                nc.scalar.activation(out=xs_of[k][:, j, :], in_=xt[:, j, :], func=ACT.Identity, bias=b)
 
         def t_add(out, xs, m, stop):
             for j in range(NB):
@@ -229,77 +260,93 @@ def tile_treelstm_pb_kernel(
                 t_add(p_of[k][:, m, :], xs_of[k], m, m == MT - 1)
 
         with tc.manual_schedule():
-            t_h("v")
-            tu(0, "s")
+            t_h(0, "v")
+            t_h(1, "s")
+            tu(0, "v")
+            tu(1, "s")
+            new_acc(0)
+            plain(0, p_of[0][:, 0, :], 0, True)
+            plain(0, p_of[0][:, 1, :], 1, False)
+            tz(0, "v")
+            tz(1, "s")
+            new_acc(1)
+            plain(1, p_of[1][:, 0, :], 0, True)
+            tw(0, 0, "v")
+            tw(0, 1, "s")
             pbias = psT.tile([P, P], BF16, name="pbias", tag="T")
             nc.tensor.transpose(pbias[:], bias_rows[:], ident_b[:])
             nc.scalar.copy(out=bias_sb[:], in_=pbias[:, 0 : 3 * KT].rearrange("p (g t) -> p t g", g=3))
-            tz(0, "v")
-            tz(1, "s")
-            new_acc(0)
-            plain(0, p_of[0][:, 0, :], 0, True)
-            tw(0, 0, "v")
-            tw(0, 1, "s")
+            plain(1, p_of[1][:, 1, :], 1, False)
             nc.vector.quantize_mx(out=zc[:].bitcast(FP8X4), scales=zs[:], in_=zgr[:])
-            plain(0, p_of[0][:, 1, :], 1, False)
             quant(0)
 
             for k in range(NS - 1):
                 prev = slice((k - 1) * P, k * P)
                 tw(k + 1, 0, "s")
-                tw(k + 1, 1, "s")
-                quant(k + 1)
+                tw(k + 1, 1, "v" if k == 4 else "s")
+                if ORDERED <= k + 2 < NS:
+                    order_words(k + 2)
                 if k >= 1:
-                    new_acc(k)
                     add_x(k - 1)
                     gi = ep.tile([P, MT, P], F32, name="gi")
                     nc.scalar.activation(out=gi[:], in_=p_of[k - 1][:, :, 0:P], func=ACT.Sigmoid)
                     gu = ep.tile([P, MT, P], F32, name="gu")
                     nc.scalar.activation(out=gu[:], in_=p_of[k - 1][:, :, P:N], func=ACT.Tanh)
-                    plain(k, p_of[k][:, 0, :], 0, True)
                     iu = ep.tile([P, MT, P], F32, name="iu")
+                    eng = nc.vector if k == NA else nc.gpsimd
+                quant(k + 1)
+                if k == 1:
+                    new_acc(2)
+                    plain(2, p_of[2][:, 0, :], 0, True)
+                if k == 2:
+                    plain(2, p_of[2][:, 1, :], 1, False)
+                if k >= 3:
+                    new_acc(k)
+                    plain(k, p_of[k][:, 0, :], 0, True)
                 xt = x_tile()
                 mm_x(k, xt)
                 if k == NA:
-                    nc.vector.tensor_tensor(out=iu[:], in0=gi[:], in1=gu[:], op=ALU.mult)
-                xs_of[k] = x_out(k, xt, "v")
+                    eng.tensor_tensor(out=iu[:], in0=gi[:], in1=gu[:], op=ALU.mult)
+                x_out(k, xt)
                 if 1 <= k < NA:
-                    nc.vector.tensor_tensor(out=iu[:], in0=gi[:], in1=gu[:], op=ALU.mult)
-                if k >= 1:
+                    eng.tensor_tensor(out=iu[:], in0=gi[:], in1=gu[:], op=ALU.mult)
+                if k >= 3:
                     plain(k, p_of[k][:, 1, :], 1, False)
+                if k == 3:
+                    absmax(0, 0, 2 * P)
                 if k >= 2:
                     cols = slice((k - 2) * P, (k - 1) * P)
                     nc.scalar.activation(out=tch[:, :, cols], in_=c_sb[:, :, cols], func=ACT.Tanh)
                 if k < NA:
-                    tu(k + 1, "v")
-                if k == NA - 1:
-                    tu(k + 2, "v")
-                if k == NA - 1:
-                    absmax(0, 0, 2 * P)
+                    tu(k + 2, "s" if k == 3 else "v")
                 if k >= 1:
-                    nc.vector.tensor_tensor(out=c_sb[:, :, prev], in0=iu[:], in1=fc_sb[:, :, prev], op=ALU.add)
+                    eng.tensor_tensor(out=c_sb[:, :, prev], in0=iu[:], in1=fc_sb[:, :, prev], op=ALU.add)
 
             nc.sync.dma_start(out=out0v[:, :, CH : 2 * CH], in_=c_sb[:])
             p5 = [psP.tile([P, N], F32, name="p5_0", tag="P"), psT.tile([P, N], F32, name="p5_1", tag="T")]
-            xt = x_tile()
+            xt = psT.tile([P, NB, MT * P], F32, name="xt5", tag="T")
             mm_x(LAST, xt)
-            xs_of[LAST] = x_out(LAST, xt, "s")
-            plain(LAST, p5[0][:], 0, True)
-            absmax(1, 2 * P, CH)
-            add_x(4)
+            xs_of[LAST] = ep.tile([P, NB, MT * P], F32, name="xs")
+            x_out_half(LAST, xt, 0, "s")
+            x_out_half(LAST, xt, 1, "v")
+            absmax(1, 2 * P, 3 * P)
+            absmax(2, 3 * P, CH)
             nc.vector.tensor_tensor(out=mab[:], in0=pmx[:, 0, :], in1=pmx[:, 1, :], op=ALU.max)
+            plain(LAST, p5[0][:], 0, True)
+            add_x(4)
             go4 = ep.tile([P, MT, N], F32, name="go4", bufs=1)
-            nc.scalar.activation(out=tch[:, :, 3 * P : CH], in_=c_sb[:, :, 3 * P : CH], func=ACT.Tanh)
             nc.scalar.activation(out=go4[:], in_=p_of[4][:], func=ACT.Sigmoid)
+            nc.scalar.activation(out=tch[:, :, 3 * P : CH], in_=c_sb[:, :, 3 * P : CH], func=ACT.Tanh)
+            t_add(p5[0][:], xs_of[LAST], 0, True)
             plain(LAST, p5[1][:], 1, True)
-            for m in range(MT):
-                t_add(p5[m][:], xs_of[LAST], m, True)
-            nc.vector.tensor_scalar(out=sc[:], in0=mab[:], scalar1=1.0 / 448.0, scalar2=None, op0=ALU.mult)
-            nc.vector.tensor_tensor(out=h_sb[:, :, 0:N], in0=go4[:], in1=tch[:, :, 0:N], op=ALU.mult)
-            nc.sync.dma_start(out=out0v[:, :, 0:N], in_=h_sb[:, :, 0:N])
+            t_add(p5[1][:], xs_of[LAST], 1, True)
+            nc.vector.tensor_tensor(out=sab[:], in0=mab[:], in1=pmx[:, 2, :], op=ALU.max)
             go5 = [ep.tile([P, N], F32, name="go5_%d" % m, bufs=1) for m in range(MT)]
             for m in range(MT):
                 nc.scalar.activation(out=go5[m][:], in_=p5[m][:], func=ACT.Sigmoid)
+            nc.vector.tensor_scalar(out=sc[:], in0=sab[:], scalar1=1.0 / 448.0, scalar2=None, op0=ALU.mult)
+            nc.vector.tensor_tensor(out=h_sb[:, :, 0:N], in0=go4[:], in1=tch[:, :, 0:N], op=ALU.mult)
+            nc.sync.dma_start(out=out0v[:, :, 0:N], in_=h_sb[:, :, 0:N])
             nc.vector.reciprocal(out=rs[:], in_=sc[:])
             for m in range(MT):
                 nc.vector.tensor_tensor(out=h_sb[:, m, N:CH], in0=go5[m][:], in1=tch[:, m, N:CH], op=ALU.mult)

@@ -25,7 +25,6 @@ N = NB * P
 NA = 4
 NS = 6
 LAST = NS - 1
-ORDERED = 3
 
 
 def tile_treelstm_pb_kernel(
@@ -44,6 +43,8 @@ def tile_treelstm_pb_kernel(
         psP = ctx.enter_context(tc.psum_pool(name="psP", bufs=3))
         psX = ctx.enter_context(tc.psum_pool(name="psX", bufs=1))
 
+        ones = const.tile([P, CH], BF16, name="ones")
+        nc.vector.memset(ones[:].bitcast(mybir.dt.int32), 0x3F803F80)
         bias_rows = const.tile([P, P], BF16, name="bias_rows")
         nc.vector.memset(bias_rows[:], 0.0)
         zcol = const.tile([P, 1], F32, name="zcol")
@@ -78,8 +79,9 @@ def tile_treelstm_pb_kernel(
         def load_u(k):
             u_in[k] = load_rows(U_i, k, 1, CH, "Ui%d" % k) + load_rows(U_u, k, 1, CH, "Uu%d" % k)
 
-        h_in = load_rows(h_tilde, 0, 1, CH, "h_in0") + load_rows(h_tilde, 1, 1, CH, "h_in1")
+        h_in = load_rows(h_tilde, 0, 1, CH, "h_in0")
         load_u(0)
+        h_in += load_rows(h_tilde, 1, 1, CH, "h_in1")
         load_u(1)
         z_in = load_rows(z0, 0, 1, SIZE, "z_in0") + load_rows(z0, 1, 1, SIZE, "z_in1")
         load_w(0)
@@ -88,15 +90,14 @@ def tile_treelstm_pb_kernel(
         load_w(1)
         load_u(2)
         load_w(2)
-        fc_sb = inp.tile([P, MT, CH], BF16, name="fc_sb")
-        nc.sync.dma_start(out=fc_sb[:], in_=fc_sum.rearrange("(m p) c -> p m c", p=P))
         load_u(3)
         load_w(3)
-        u_o = load_rows(U_o, 0, 2 * NB, CH, "Uo")
-        u_in[NA] = u_o[0:NB]
-        u_in[NA + 1] = u_o[NB : 2 * NB]
-        load_w(NA)
-        load_w(NA + 1)
+        fc_sb = inp.tile([P, MT, CH], BF16, name="fc_sb")
+        nc.sync.dma_start(out=fc_sb[:], in_=fc_sum.rearrange("(m p) c -> p m c", p=P))
+        load_w(4)
+        u_in[NA] = load_rows(U_o, 0, NB, CH, "Uo0")
+        load_w(5)
+        u_in[NA + 1] = load_rows(U_o, NB, NB, CH, "Uo1")
 
         hT = keep.tile([P, MT, 2, P, 2], BF16, name="hT")
         zgr = keep.tile([P, NPASS * MT * P * 4], BF16, name="zgr", align_bytes=64)
@@ -114,7 +115,8 @@ def tile_treelstm_pb_kernel(
         qc = keep.tile([P, MT, CH], FP8, name="qc")
         qh = keep.tile([P, MT, CH], FP8, name="qh")
         uT = [keep.tile([P, 2, N, 2], BF16, name="uT%d" % k) for k in range(NS)]
-        wo = {k: keep.tile([P, NB, NPASS, 2, P], F32, name="wo%d" % k) for k in range(ORDERED, NS)}
+        wo = {k: keep.tile([P, NB, NPASS, 2, P], F32, name="wo%d" % k) for k in [2,3,4,5]}
+        zo = keep.tile([P, MT, NPASS, 2, P], F32, name="zo")
         wgr = [keep.tile([P, NPASS * N * 4], BF16, name="wgr%d" % k, align_bytes=64) for k in range(NS)]
         wc = [keep.tile([P, NPASS * N], U32, name="wc%d" % k, align_bytes=64) for k in range(NS)]
         ws = [keep.tile([P, NPASS * N], U8, name="ws%d" % k, align_bytes=64) for k in range(NS)]
@@ -132,38 +134,51 @@ def tile_treelstm_pb_kernel(
                 nc.tensor.transpose(pt[:, j, :], words[:, j * P : (j + 1) * P], ident_f[:])
             copy_out(eng, hT[:, m].rearrange("p j r e -> p (j r e)").bitcast(F32), pt[:].rearrange("p j r -> p (j r)"))
 
-        def t_words(src, dst, eng):
-            words = src.bitcast(F32)
-            pw = psT.tile([P, NPASS, 2, P], F32, name="pw", tag="T")
-            for g in range(NPASS):
-                for u in range(2):
-                    nc.tensor.transpose(
-                        pw[:, g, u, :], words[:, 256 * g + u : 256 * (g + 1) : 2], ident_f[:]
-                    )
-            copy_out(eng, dst, pw[:].rearrange("p g u c -> p g c u"))
-
         def word_view(t):
             return t[:].bitcast(F32).rearrange("p (g c u) -> p g c u", g=NPASS, u=2)
 
-        def tz(m, eng):
-            t_words(z_in[m], word_view(zgr)[:, :, m * P : (m + 1) * P, :], eng)
+        def order_words(t, j, src, eng):
+            copy_out(
+                eng,
+                t[:, j].rearrange("p g u q -> p g u q"),
+                src.bitcast(F32).rearrange("p (g q u) -> p g u q", g=NPASS, u=2),
+            )
 
-        def order_words(k):
+        def order_pair(k):
             nc.vector.tensor_copy(
                 out=wo[k][:].rearrange("p j g u q -> p (j g) u q"),
                 in_=w_in[k][:].bitcast(F32).rearrange("p j (g q u) -> p (j g) u q", g=NPASS, u=2),
             )
 
+        def t_words(words, dst, eng):
+            pw = psT.tile([P, NPASS, 2, P], F32, name="pw", tag="T")
+            for g in range(NPASS):
+                for u in range(2):
+                    nc.tensor.transpose(pw[:, g, u, :], words(g, u), ident_f[:])
+            copy_out(eng, dst, pw[:].rearrange("p g u c -> p g c u"))
+
+        def stepped(src):
+            w = src.bitcast(F32)
+            return lambda g, u: w[:, 256 * g + u : 256 * (g + 1) : 2]
+
+        def ordered(t, j):
+            return lambda g, u: t[:, j, g, u, :]
+
+        def tz(m, eng):
+            dst = word_view(zgr)[:, :, m * P : (m + 1) * P, :]
+            t_words(ordered(zo, m) if True else stepped(z_in[m]), dst, eng)
+
         def tw(k, j, eng):
             dst = word_view(wgr[k])[:, :, j * P : (j + 1) * P, :]
-            if k < ORDERED:
-                t_words(w_in[k][:, j, :], dst, eng)
-            else:
-                pw = psT.tile([P, NPASS, 2, P], F32, name="pw", tag="T")
-                for g in range(NPASS):
-                    for u in range(2):
-                        nc.tensor.transpose(pw[:, g, u, :], wo[k][:, j, g, u, :], ident_f[:])
-                copy_out(eng, dst, pw[:].rearrange("p g u c -> p g c u"))
+            t_words(ordered(wo[k], j) if k in wo else stepped(w_in[k][:, j, :]), dst, eng)
+
+        def tu_half(k, b, eng):
+            pu = psT.tile([P, 2, P], F32, name="pu_half", tag="T")
+            words = u_in[k][b].bitcast(F32)
+            for j in range(2):
+                nc.tensor.transpose(pu[:, j, :], words[:, j * P : (j + 1) * P], ident_f[:])
+            dst = uT[k][:].rearrange("p j c e -> p (j c e)").bitcast(F32).rearrange("p (j b c) -> p j b c", j=2, b=NB)
+            copy_out(eng, dst[:, :, b, :], pu[:])
 
         def tu(k, eng):
             pu = psT.tile([P, NB, 2, P], F32, name="pu", tag="T")
@@ -260,13 +275,19 @@ def tile_treelstm_pb_kernel(
                 t_add(p_of[k][:, m, :], xs_of[k], m, m == MT - 1)
 
         with tc.manual_schedule():
+            warm_ps = psT.tile([P, CH], F32, name="warm_ps", tag="T")
+            for i in range(3):
+                nc.tensor.matmul(out=warm_ps[:], lhsT=ones[:, 0:P], rhs=ones[:], start=True, stop=True)
             t_h(0, "v")
-            t_h(1, "s")
-            tu(0, "v")
+            tu_half(0, 0, "v")
+            tu_half(0, 1, "s")
+            t_h(1, "v")
             tu(1, "s")
             new_acc(0)
             plain(0, p_of[0][:, 0, :], 0, True)
             plain(0, p_of[0][:, 1, :], 1, False)
+            order_words(zo, 0, z_in[0], "v")
+            order_words(zo, 1, z_in[1], "v")
             tz(0, "v")
             tz(1, "s")
             new_acc(1)
@@ -284,8 +305,8 @@ def tile_treelstm_pb_kernel(
                 prev = slice((k - 1) * P, k * P)
                 tw(k + 1, 0, "s")
                 tw(k + 1, 1, "v" if k == 4 else "s")
-                if ORDERED <= k + 2 < NS:
-                    order_words(k + 2)
+                if k + 2 in wo and k != 9:
+                    order_pair(k + 2)
                 if k >= 1:
                     add_x(k - 1)
                     gi = ep.tile([P, MT, P], F32, name="gi")
@@ -294,7 +315,8 @@ def tile_treelstm_pb_kernel(
                     nc.scalar.activation(out=gu[:], in_=p_of[k - 1][:, :, P:N], func=ACT.Tanh)
                     iu = ep.tile([P, MT, P], F32, name="iu")
                     eng = nc.vector if k == NA else nc.gpsimd
-                quant(k + 1)
+                if k >= 1:
+                    quant(k + 1)
                 if k == 1:
                     new_acc(2)
                     plain(2, p_of[2][:, 0, :], 0, True)
@@ -307,7 +329,16 @@ def tile_treelstm_pb_kernel(
                 mm_x(k, xt)
                 if k == NA:
                     eng.tensor_tensor(out=iu[:], in0=gi[:], in1=gu[:], op=ALU.mult)
-                x_out(k, xt)
+                if k == NA:
+                    xs_of[k] = ep.tile([P, NB, MT * P], F32, name="xs")
+                    x_out_half(k, xt, 0, "s")
+                    x_out_half(k, xt, 1, "s")
+                else:
+                    x_out(k, xt)
+                if k < 1:
+                    quant(k + 1)
+                if k + 2 in wo and k == 9:
+                    order_pair(k + 2)
                 if 1 <= k < NA:
                     eng.tensor_tensor(out=iu[:], in0=gi[:], in1=gu[:], op=ALU.mult)
                 if k >= 3:
@@ -318,7 +349,7 @@ def tile_treelstm_pb_kernel(
                     cols = slice((k - 2) * P, (k - 1) * P)
                     nc.scalar.activation(out=tch[:, :, cols], in_=c_sb[:, :, cols], func=ACT.Tanh)
                 if k < NA:
-                    tu(k + 2, "s" if k == 3 else "v")
+                    tu(k + 2, "s" if k in (0, 3) else "v")
                 if k >= 1:
                     eng.tensor_tensor(out=c_sb[:, :, prev], in0=iu[:], in1=fc_sb[:, :, prev], op=ALU.add)
 
@@ -329,22 +360,22 @@ def tile_treelstm_pb_kernel(
             xs_of[LAST] = ep.tile([P, NB, MT * P], F32, name="xs")
             x_out_half(LAST, xt, 0, "s")
             x_out_half(LAST, xt, 1, "v")
-            absmax(1, 2 * P, 3 * P)
-            absmax(2, 3 * P, CH)
-            nc.vector.tensor_tensor(out=mab[:], in0=pmx[:, 0, :], in1=pmx[:, 1, :], op=ALU.max)
-            plain(LAST, p5[0][:], 0, True)
+            absmax(1, 2 * P, CH)
             add_x(4)
+            plain(LAST, p5[0][:], 0, True)
+            nc.vector.tensor_scalar(out=sab[:], in0=pmx[:, 0, :], scalar1=1.0 / 448.0, scalar2=None, op0=ALU.mult)
+            nc.scalar.activation(out=tch[:, :, 3 * P : CH], in_=c_sb[:, :, 3 * P : CH], func=ACT.Tanh)
             go4 = ep.tile([P, MT, N], F32, name="go4", bufs=1)
             nc.scalar.activation(out=go4[:], in_=p_of[4][:], func=ACT.Sigmoid)
-            nc.scalar.activation(out=tch[:, :, 3 * P : CH], in_=c_sb[:, :, 3 * P : CH], func=ACT.Tanh)
             t_add(p5[0][:], xs_of[LAST], 0, True)
             plain(LAST, p5[1][:], 1, True)
             t_add(p5[1][:], xs_of[LAST], 1, True)
-            nc.vector.tensor_tensor(out=sab[:], in0=mab[:], in1=pmx[:, 2, :], op=ALU.max)
             go5 = [ep.tile([P, N], F32, name="go5_%d" % m, bufs=1) for m in range(MT)]
             for m in range(MT):
                 nc.scalar.activation(out=go5[m][:], in_=p5[m][:], func=ACT.Sigmoid)
-            nc.vector.tensor_scalar(out=sc[:], in0=sab[:], scalar1=1.0 / 448.0, scalar2=None, op0=ALU.mult)
+            nc.vector.scalar_tensor_tensor(
+                out=sc[:], in0=pmx[:, 1, :], scalar=1.0 / 448.0, in1=sab[:], op0=ALU.mult, op1=ALU.max
+            )
             nc.vector.tensor_tensor(out=h_sb[:, :, 0:N], in0=go4[:], in1=tch[:, :, 0:N], op=ALU.mult)
             nc.sync.dma_start(out=out0v[:, :, 0:N], in_=h_sb[:, :, 0:N])
             nc.vector.reciprocal(out=rs[:], in_=sc[:])

@@ -51,10 +51,10 @@ def tile_treelstm_pb_kernel(
         nc.vector.memset(zcol[:], 0.0)
         warm = const.tile([P, 1], F32, name="warm")
         nc.scalar.activation(out=warm[:], in_=zcol[:], func=ACT.Sigmoid)
-        ident_f = const.tile([P, P], F32, name="ident_f")
-        make_identity(nc, ident_f[:])
         ident_b = const.tile([P, P], BF16, name="ident_b")
         make_identity(nc, ident_b[:])
+        ident_f = const.tile([P, P], F32, name="ident_f")
+        make_identity(nc, ident_f[:])
 
         def load_rows(dram, r0, nrt, width, name):
             t = inp.tile([P, nrt, width], BF16, name=name)
@@ -99,7 +99,7 @@ def tile_treelstm_pb_kernel(
         load_w(5)
         u_in[NA + 1] = load_rows(U_o, NB, NB, CH, "Uo1")
 
-        hT = keep.tile([P, MT, 2, P, 2], BF16, name="hT")
+        hT = keep.tile([P, MT, KT, P], BF16, name="hT")
         zgr = keep.tile([P, NPASS * MT * P * 4], BF16, name="zgr", align_bytes=64)
         zc = keep.tile([P, NPASS * MT * P], U32, name="zc", align_bytes=64)
         zs = keep.tile([P, NPASS * MT * P], U8, name="zs", align_bytes=64)
@@ -128,11 +128,11 @@ def tile_treelstm_pb_kernel(
                 nc.scalar.copy(out=out, in_=in_)
 
         def t_h(m, eng):
-            pt = psT.tile([P, 2, P], F32, name="pt", tag="T")
-            words = h_in[m].bitcast(F32)
-            for j in range(2):
-                nc.tensor.transpose(pt[:, j, :], words[:, j * P : (j + 1) * P], ident_f[:])
-            copy_out(eng, hT[:, m].rearrange("p j r e -> p (j r e)").bitcast(F32), pt[:].rearrange("p j r -> p (j r)"))
+            pt = psT.tile([P, KT, P], BF16, name="pt", tag="T")
+            for kt in range(KT):
+                j, e = divmod(kt, 2)
+                nc.tensor.transpose(pt[:, kt, :], h_in[m][:, 256 * j + e : 256 * (j + 1) : 2], ident_b[:])
+            copy_out(eng, hT[:, m], pt[:])
 
         def word_view(t):
             return t[:].bitcast(F32).rearrange("p (g c u) -> p g c u", g=NPASS, u=2)
@@ -194,7 +194,7 @@ def tile_treelstm_pb_kernel(
 
         def mm_p(k, out, m, kt, start):
             nc.tensor.matmul(
-                out=out, lhsT=hT[:, m, kt // 2, :, kt % 2], rhs=uT[k][:, kt // 2, :, kt % 2], start=start, stop=False
+                out=out, lhsT=hT[:, m, kt, :], rhs=uT[k][:, kt // 2, :, kt % 2], start=start, stop=False
             )
 
         def mm_x(k, xt):

@@ -257,8 +257,8 @@ def tile_treelstm_pb_kernel(
                     out=out, in_=in_, func=ACT.Identity, scale=rs[:, m : m + 1], bias=zcol[:, 0:1], saturate=False
                 )
 
-        def plain(k, out, m, start):
-            for kt in range(KT):
+        def plain(k, out, m, start, kts=range(KT)):
+            for kt in kts:
                 mm_p(k, out, m, kt, start and kt == 0)
 
         p_of = {}
@@ -291,21 +291,23 @@ def tile_treelstm_pb_kernel(
             tz(0, "v")
             tz(1, "s")
             new_acc(1)
-            plain(1, p_of[1][:, 0, :], 0, True)
             tw(0, 0, "v")
+            plain(1, p_of[1][:, 0, :], 0, True, (0, 1))
             tw(0, 1, "s")
+            plain(1, p_of[1][:, 0, :], 0, True, (2, 3))
             pbias = psT.tile([P, P], BF16, name="pbias", tag="T")
             nc.tensor.transpose(pbias[:], bias_rows[:], ident_b[:])
             nc.scalar.copy(out=bias_sb[:], in_=pbias[:, 0 : 3 * KT].rearrange("p (g t) -> p t g", g=3))
-            plain(1, p_of[1][:, 1, :], 1, False)
             nc.vector.quantize_mx(out=zc[:].bitcast(FP8X4), scales=zs[:], in_=zgr[:])
             quant(0)
 
-            for k in range(NS - 1):
+            for k in range(NA):
                 prev = slice((k - 1) * P, k * P)
                 tw(k + 1, 0, "s")
-                tw(k + 1, 1, "v" if k == 4 else "s")
-                if k + 2 in wo and k != 9:
+                if k == 0:
+                    plain(1, p_of[1][:, 1, :], 1, False, (0, 1))
+                tw(k + 1, 1, "s")
+                if k + 2 < NS:
                     order_pair(k + 2)
                 if k >= 1:
                     add_x(k - 1)
@@ -314,45 +316,49 @@ def tile_treelstm_pb_kernel(
                     gu = ep.tile([P, MT, P], F32, name="gu")
                     nc.scalar.activation(out=gu[:], in_=p_of[k - 1][:, :, P:N], func=ACT.Tanh)
                     iu = ep.tile([P, MT, P], F32, name="iu")
-                    eng = nc.vector if k == NA else nc.gpsimd
-                if k >= 1:
-                    quant(k + 1)
-                if k == 1:
-                    new_acc(2)
-                    plain(2, p_of[2][:, 0, :], 0, True)
-                if k == 2:
-                    plain(2, p_of[2][:, 1, :], 1, False)
-                if k >= 3:
-                    new_acc(k)
-                    plain(k, p_of[k][:, 0, :], 0, True)
+                pk, pm = ((1, 1), (2, 0), (2, 1), (3, 0))[k]
+                if pm == 0:
+                    new_acc(pk)
+                plain(pk, p_of[pk][:, pm, :], pm, pm == 0, (2,) if k == 0 else (0, 1))
                 xt = x_tile()
                 mm_x(k, xt)
-                if k == NA:
-                    eng.tensor_tensor(out=iu[:], in0=gi[:], in1=gu[:], op=ALU.mult)
-                if k == NA:
-                    xs_of[k] = ep.tile([P, NB, MT * P], F32, name="xs")
-                    x_out_half(k, xt, 0, "s")
-                    x_out_half(k, xt, 1, "s")
-                else:
-                    x_out(k, xt)
-                if k < 1:
-                    quant(k + 1)
-                if k + 2 in wo and k == 9:
-                    order_pair(k + 2)
-                if 1 <= k < NA:
-                    eng.tensor_tensor(out=iu[:], in0=gi[:], in1=gu[:], op=ALU.mult)
-                if k >= 3:
-                    plain(k, p_of[k][:, 1, :], 1, False)
+                x_out(k, xt)
+                plain(pk, p_of[pk][:, pm, :], pm, pm == 0, (3,) if k == 0 else (2, 3))
+                quant(k + 1)
                 if k == 3:
-                    absmax(0, 0, 2 * P)
+                    plain(3, p_of[3][:, 1, :], 1, False)
+                if k >= 1:
+                    nc.vector.tensor_tensor(out=iu[:], in0=gi[:], in1=gu[:], op=ALU.mult)
                 if k >= 2:
                     cols = slice((k - 2) * P, (k - 1) * P)
                     nc.scalar.activation(out=tch[:, :, cols], in_=c_sb[:, :, cols], func=ACT.Tanh)
-                if k < NA:
-                    tu(k + 2, "s" if k in (0, 3) else "v")
-                if k >= 1:
-                    eng.tensor_tensor(out=c_sb[:, :, prev], in0=iu[:], in1=fc_sb[:, :, prev], op=ALU.add)
+                if k < 3:
+                    tu(k + 2, "s")
+                if 1 <= k < 3:
+                    nc.vector.tensor_tensor(out=c_sb[:, :, prev], in0=iu[:], in1=fc_sb[:, :, prev], op=ALU.add)
 
+            iu2 = iu
+            tw(5, 0, "s")
+            tw(5, 1, "v")
+            quant(5)
+            add_x(3)
+            gi = ep.tile([P, MT, P], F32, name="gi")
+            nc.scalar.activation(out=gi[:], in_=p_of[3][:, :, 0:P], func=ACT.Sigmoid)
+            gu = ep.tile([P, MT, P], F32, name="gu")
+            nc.scalar.activation(out=gu[:], in_=p_of[3][:, :, P:N], func=ACT.Tanh)
+            tu(5, "s")
+            new_acc(4)
+            plain(4, p_of[4][:, 0, :], 0, True)
+            xt = x_tile()
+            mm_x(4, xt)
+            iu = ep.tile([P, MT, P], F32, name="iu")
+            nc.vector.tensor_tensor(out=iu[:], in0=gi[:], in1=gu[:], op=ALU.mult)
+            nc.vector.tensor_tensor(out=c_sb[:, :, 2 * P : 3 * P], in0=iu2[:], in1=fc_sb[:, :, 2 * P : 3 * P], op=ALU.add)
+            nc.vector.tensor_tensor(out=c_sb[:, :, 3 * P : CH], in0=iu[:], in1=fc_sb[:, :, 3 * P : CH], op=ALU.add)
+            xs_of[4] = ep.tile([P, NB, MT * P], F32, name="xs")
+            x_out_half(4, xt, 0, "s")
+            x_out_half(4, xt, 1, "s")
+            plain(4, p_of[4][:, 1, :], 1, False)
             nc.sync.dma_start(out=out0v[:, :, CH : 2 * CH], in_=c_sb[:])
             p5 = [psP.tile([P, N], F32, name="p5_0", tag="P"), psT.tile([P, N], F32, name="p5_1", tag="T")]
             xt = psT.tile([P, NB, MT * P], F32, name="xt5", tag="T")
@@ -360,24 +366,25 @@ def tile_treelstm_pb_kernel(
             xs_of[LAST] = ep.tile([P, NB, MT * P], F32, name="xs")
             x_out_half(LAST, xt, 0, "s")
             x_out_half(LAST, xt, 1, "v")
+            absmax(0, 0, 2 * P)
             absmax(1, 2 * P, CH)
             add_x(4)
             plain(LAST, p5[0][:], 0, True)
-            nc.vector.tensor_scalar(out=sab[:], in0=pmx[:, 0, :], scalar1=1.0 / 448.0, scalar2=None, op0=ALU.mult)
-            nc.scalar.activation(out=tch[:, :, 3 * P : CH], in_=c_sb[:, :, 3 * P : CH], func=ACT.Tanh)
             go4 = ep.tile([P, MT, N], F32, name="go4", bufs=1)
             nc.scalar.activation(out=go4[:], in_=p_of[4][:], func=ACT.Sigmoid)
+            nc.scalar.activation(out=tch[:, :, 2 * P : CH], in_=c_sb[:, :, 2 * P : CH], func=ACT.Tanh)
+            nc.vector.tensor_scalar(out=sab[:], in0=pmx[:, 0, :], scalar1=1.0 / 448.0, scalar2=None, op0=ALU.mult)
             t_add(p5[0][:], xs_of[LAST], 0, True)
             plain(LAST, p5[1][:], 1, True)
             t_add(p5[1][:], xs_of[LAST], 1, True)
-            go5 = [ep.tile([P, N], F32, name="go5_%d" % m, bufs=1) for m in range(MT)]
-            for m in range(MT):
-                nc.scalar.activation(out=go5[m][:], in_=p5[m][:], func=ACT.Sigmoid)
             nc.vector.scalar_tensor_tensor(
                 out=sc[:], in0=pmx[:, 1, :], scalar=1.0 / 448.0, in1=sab[:], op0=ALU.mult, op1=ALU.max
             )
             nc.vector.tensor_tensor(out=h_sb[:, :, 0:N], in0=go4[:], in1=tch[:, :, 0:N], op=ALU.mult)
             nc.sync.dma_start(out=out0v[:, :, 0:N], in_=h_sb[:, :, 0:N])
+            go5 = [ep.tile([P, N], F32, name="go5_%d" % m, bufs=1) for m in range(MT)]
+            for m in range(MT):
+                nc.scalar.activation(out=go5[m][:], in_=p5[m][:], func=ACT.Sigmoid)
             nc.vector.reciprocal(out=rs[:], in_=sc[:])
             for m in range(MT):
                 nc.vector.tensor_tensor(out=h_sb[:, m, N:CH], in0=go5[m][:], in1=tch[:, m, N:CH], op=ALU.mult)

@@ -31,8 +31,8 @@ def tile_treelstm_pb_kernel(
     tc, z0, h_tilde, fc_sum, W_i, U_i, b_i, W_o, U_o, b_o, W_u, U_u, b_u, out_0, out_1
 ):
     nc = tc.nc
-    out0v = out_0.rearrange("(m p) n -> p m n", p=P)
-    out1v = out_1.rearrange("(m p) n -> p m n", p=P)
+    out0v = out_0.rearrange("(p m) n -> p m n", p=P)
+    out1v = out_1.rearrange("(p m) n -> p m n", p=P)
 
     with ExitStack() as ctx:
         const = ctx.enter_context(tc.tile_pool(name="const", bufs=1))
@@ -47,6 +47,8 @@ def tile_treelstm_pb_kernel(
         nc.vector.memset(ones[:].bitcast(mybir.dt.int32), 0x3F803F80)
         bias_rows = const.tile([P, P], BF16, name="bias_rows")
         nc.vector.memset(bias_rows[:], 0.0)
+        bo_rows = const.tile([P, N], BF16, name="bo_rows")
+        nc.vector.memset(bo_rows[:], 0.0)
         zcol = const.tile([P, 1], F32, name="zcol")
         nc.vector.memset(zcol[:], 0.0)
         warm = const.tile([P, 1], F32, name="warm")
@@ -59,7 +61,7 @@ def tile_treelstm_pb_kernel(
         def load_rows(dram, r0, nrt, width, name):
             t = inp.tile([P, nrt, width], BF16, name=name)
             nc.sync.dma_start(
-                out=t[:], in_=dram[r0 * P : (r0 + nrt) * P, :].rearrange("(t p) k -> p t k", p=P)
+                out=t[:], in_=dram[r0 * P : (r0 + nrt) * P, :].rearrange("(p t) k -> p t k", p=P)
             )
             return [t[:, j, :] for j in range(nrt)]
 
@@ -73,27 +75,27 @@ def tile_treelstm_pb_kernel(
                     nc.sync.dma_start(out=t[:, j, :], in_=W[k * P : (k + 1) * P, :])
             else:
                 r0 = (k - NA) * N
-                nc.sync.dma_start(out=t[:], in_=W_o[r0 : r0 + N, :].rearrange("(t p) k -> p t k", p=P))
+                nc.sync.dma_start(out=t[:], in_=W_o[r0 : r0 + N, :].rearrange("(p t) k -> p t k", p=P))
             w_in[k] = t
 
         def load_u(k):
             u_in[k] = load_rows(U_i, k, 1, CH, "Ui%d" % k) + load_rows(U_u, k, 1, CH, "Uu%d" % k)
 
-        h_in = load_rows(h_tilde, 0, 1, CH, "h_in0")
+        h_in = load_rows(h_tilde, 0, MT, CH, "h_in")
         load_u(0)
-        h_in += load_rows(h_tilde, 1, 1, CH, "h_in1")
         load_u(1)
-        z_in = load_rows(z0, 0, 1, SIZE, "z_in0") + load_rows(z0, 1, 1, SIZE, "z_in1")
+        z_in = load_rows(z0, 0, MT, SIZE, "z_in")
         load_w(0)
-        for j, b in enumerate((b_i, b_u, b_o)):
+        for j, b in enumerate((b_i, b_u)):
             nc.sync.dma_start(out=bias_rows[j * KT : (j + 1) * KT, :], in_=b.rearrange("(t c) -> t c", c=P))
+        nc.sync.dma_start(out=bo_rows[0:2, :], in_=b_o.rearrange("(s c) -> s c", c=N))
         load_w(1)
         load_u(2)
         load_w(2)
-        load_u(3)
         load_w(3)
+        load_u(3)
         fc_sb = inp.tile([P, MT, CH], BF16, name="fc_sb")
-        nc.sync.dma_start(out=fc_sb[:], in_=fc_sum.rearrange("(m p) c -> p m c", p=P))
+        nc.sync.dma_start(out=fc_sb[:], in_=fc_sum.rearrange("(p m) c -> p m c", p=P))
         load_w(4)
         u_in[NA] = load_rows(U_o, 0, NB, CH, "Uo0")
         load_w(5)
@@ -103,7 +105,7 @@ def tile_treelstm_pb_kernel(
         zgr = keep.tile([P, NPASS * MT * P * 4], BF16, name="zgr", align_bytes=64)
         zc = keep.tile([P, NPASS * MT * P], U32, name="zc", align_bytes=64)
         zs = keep.tile([P, NPASS * MT * P], U8, name="zs", align_bytes=64)
-        bias_sb = keep.tile([P, KT, 3], F32, name="bias_sb")
+        bias_sb = keep.tile([P, NS, NB], F32, name="bias_sb")
         c_sb = keep.tile([P, MT, CH], F32, name="c_sb")
         tch = keep.tile([P, MT, CH], F32, name="tch")
         h_sb = keep.tile([P, MT, CH], F32, name="h_sb")
@@ -213,7 +215,7 @@ def tile_treelstm_pb_kernel(
                     )
 
         def x_bias(k):
-            return bias_sb[:, k, 0:NB] if k < NA else bias_sb[:, (k - NA) * NB : (k - NA + 1) * NB, 2]
+            return bias_sb[:, k, :]
 
         def x_out(k, xt):
             xs_of[k] = ep.tile([P, NB, MT * P], F32, name="xs")
@@ -295,9 +297,12 @@ def tile_treelstm_pb_kernel(
             plain(1, p_of[1][:, 0, :], 0, True, (0, 1))
             tw(0, 1, "s")
             plain(1, p_of[1][:, 0, :], 0, True, (2, 3))
-            pbias = psT.tile([P, P], BF16, name="pbias", tag="T")
-            nc.tensor.transpose(pbias[:], bias_rows[:], ident_b[:])
-            nc.scalar.copy(out=bias_sb[:], in_=pbias[:, 0 : 3 * KT].rearrange("p (g t) -> p t g", g=3))
+            pbias = psT.tile([P, 3, P], BF16, name="pbias", tag="T")
+            nc.tensor.transpose(pbias[:, 0, :], bias_rows[:], ident_b[:])
+            for j in range(NB):
+                nc.tensor.transpose(pbias[:, 1 + j, :], bo_rows[:, j:N:2], ident_b[:])
+            nc.scalar.copy(out=bias_sb[:, 0:NA, :], in_=pbias[:, 0, 0 : NB * KT].rearrange("p (g t) -> p t g", g=NB))
+            nc.scalar.copy(out=bias_sb[:, NA:NS, :], in_=pbias[:, 1 : 1 + NB, 0 : NS - NA].rearrange("p j s -> p s j"))
             nc.vector.quantize_mx(out=zc[:].bitcast(FP8X4), scales=zs[:], in_=zgr[:])
             quant(0)
 
@@ -316,24 +321,27 @@ def tile_treelstm_pb_kernel(
                     gu = ep.tile([P, MT, P], F32, name="gu")
                     nc.scalar.activation(out=gu[:], in_=p_of[k - 1][:, :, P:N], func=ACT.Tanh)
                     iu = ep.tile([P, MT, P], F32, name="iu")
-                pk, pm = ((1, 1), (2, 0), (2, 1), (3, 0))[k]
-                if pm == 0:
+                pk, pm = ((1, 1), (2, 1), (3, 0), (3, 1))[k]
+                if pk == 3 and pm == 0:
                     new_acc(pk)
+                if k == 0:
+                    tu(2, "s")
                 plain(pk, p_of[pk][:, pm, :], pm, pm == 0, (2,) if k == 0 else (0, 1))
                 xt = x_tile()
                 mm_x(k, xt)
                 x_out(k, xt)
                 plain(pk, p_of[pk][:, pm, :], pm, pm == 0, (3,) if k == 0 else (2, 3))
                 quant(k + 1)
-                if k == 3:
-                    plain(3, p_of[3][:, 1, :], 1, False)
+                if k == 0:
+                    new_acc(2)
+                    plain(2, p_of[2][:, 0, :], 0, True)
                 if k >= 1:
                     nc.vector.tensor_tensor(out=iu[:], in0=gi[:], in1=gu[:], op=ALU.mult)
                 if k >= 2:
                     cols = slice((k - 2) * P, (k - 1) * P)
                     nc.scalar.activation(out=tch[:, :, cols], in_=c_sb[:, :, cols], func=ACT.Tanh)
-                if k < 3:
-                    tu(k + 2, "s")
+                if k in (1, 3):
+                    tu(3 if k == 1 else 4, "s")
                 if 1 <= k < 3:
                     nc.vector.tensor_tensor(out=c_sb[:, :, prev], in0=iu[:], in1=fc_sb[:, :, prev], op=ALU.add)
 
@@ -365,13 +373,17 @@ def tile_treelstm_pb_kernel(
             mm_x(LAST, xt)
             xs_of[LAST] = ep.tile([P, NB, MT * P], F32, name="xs")
             x_out_half(LAST, xt, 0, "s")
-            x_out_half(LAST, xt, 1, "v")
+            x_out_half(LAST, xt, 1, "s")
             absmax(0, 0, 2 * P)
             absmax(1, 2 * P, CH)
             add_x(4)
             plain(LAST, p5[0][:], 0, True)
             go4 = ep.tile([P, MT, N], F32, name="go4", bufs=1)
-            nc.scalar.activation(out=go4[:], in_=p_of[4][:], func=ACT.Sigmoid)
+            nc.scalar.activation(
+                out=go4[:].rearrange("p m (q j) -> p m q j", j=NB),
+                in_=p_of[4][:].rearrange("p m (j q) -> p m q j", j=NB),
+                func=ACT.Sigmoid,
+            )
             nc.scalar.activation(out=tch[:, :, 2 * P : CH], in_=c_sb[:, :, 2 * P : CH], func=ACT.Tanh)
             nc.vector.tensor_scalar(out=sab[:], in0=pmx[:, 0, :], scalar1=1.0 / 448.0, scalar2=None, op0=ALU.mult)
             t_add(p5[0][:], xs_of[LAST], 0, True)
@@ -384,7 +396,11 @@ def tile_treelstm_pb_kernel(
             nc.sync.dma_start(out=out0v[:, :, 0:N], in_=h_sb[:, :, 0:N])
             go5 = [ep.tile([P, N], F32, name="go5_%d" % m, bufs=1) for m in range(MT)]
             for m in range(MT):
-                nc.scalar.activation(out=go5[m][:], in_=p5[m][:], func=ACT.Sigmoid)
+                nc.scalar.activation(
+                    out=go5[m][:].rearrange("p (q j) -> p q j", j=NB),
+                    in_=p5[m][:].rearrange("p (j q) -> p q j", j=NB),
+                    func=ACT.Sigmoid,
+                )
             nc.vector.reciprocal(out=rs[:], in_=sc[:])
             for m in range(MT):
                 nc.vector.tensor_tensor(out=h_sb[:, m, N:CH], in0=go5[m][:], in1=tch[:, m, N:CH], op=ALU.mult)

@@ -117,7 +117,7 @@ def tile_treelstm_pb_kernel(
         qc = keep.tile([P, MT, CH], FP8, name="qc")
         qh = keep.tile([P, MT, CH], FP8, name="qh")
         uT = [keep.tile([P, 2, N, 2], BF16, name="uT%d" % k) for k in range(NS)]
-        wo = {k: keep.tile([P, NB, NPASS, 2, P], F32, name="wo%d" % k) for k in [2,3,4,5]}
+        wo = {k: keep.tile([P, NB, NPASS, 2, P], F32, name="wo%d" % k) for k in [0,2,3,4,5]}
         zo = keep.tile([P, MT, NPASS, 2, P], F32, name="zo")
         wgr = [keep.tile([P, NPASS * N * 4], BF16, name="wgr%d" % k, align_bytes=64) for k in range(NS)]
         wc = [keep.tile([P, NPASS * N], U32, name="wc%d" % k, align_bytes=64) for k in range(NS)]
@@ -290,13 +290,15 @@ def tile_treelstm_pb_kernel(
             plain(0, p_of[0][:, 1, :], 1, False)
             order_words(zo, 0, z_in[0], "v")
             order_words(zo, 1, z_in[1], "v")
+            order_words(wo[0], 0, w_in[0][:, 0, :], "s")
             tz(0, "v")
             tz(1, "s")
+            order_words(wo[0], 1, w_in[0][:, 1, :], "v")
             new_acc(1)
-            tw(0, 0, "v")
             plain(1, p_of[1][:, 0, :], 0, True, (0, 1))
-            tw(0, 1, "s")
+            tw(0, 0, "v")
             plain(1, p_of[1][:, 0, :], 0, True, (2, 3))
+            tw(0, 1, "s")
             pbias = psT.tile([P, 3, P], BF16, name="pbias", tag="T")
             nc.tensor.transpose(pbias[:, 0, :], bias_rows[:], ident_b[:])
             for j in range(NB):
@@ -306,74 +308,102 @@ def tile_treelstm_pb_kernel(
             nc.vector.quantize_mx(out=zc[:].bitcast(FP8X4), scales=zs[:], in_=zgr[:])
             quant(0)
 
-            for k in range(NA):
-                prev = slice((k - 1) * P, k * P)
-                tw(k + 1, 0, "s")
-                if k == 0:
-                    plain(1, p_of[1][:, 1, :], 1, False, (0, 1))
-                tw(k + 1, 1, "s")
-                if k + 2 < NS:
-                    order_pair(k + 2)
-                if k >= 1:
-                    add_x(k - 1)
-                    gi = ep.tile([P, MT, P], F32, name="gi")
-                    nc.scalar.activation(out=gi[:], in_=p_of[k - 1][:, :, 0:P], func=ACT.Sigmoid)
-                    gu = ep.tile([P, MT, P], F32, name="gu")
-                    nc.scalar.activation(out=gu[:], in_=p_of[k - 1][:, :, P:N], func=ACT.Tanh)
-                    iu = ep.tile([P, MT, P], F32, name="iu")
-                pk, pm = ((1, 1), (2, 1), (3, 0), (3, 1))[k]
-                if pk == 3 and pm == 0:
-                    new_acc(pk)
-                if k == 0:
-                    tu(2, "s")
-                plain(pk, p_of[pk][:, pm, :], pm, pm == 0, (2,) if k == 0 else (0, 1))
-                xt = x_tile()
-                mm_x(k, xt)
-                x_out(k, xt)
-                plain(pk, p_of[pk][:, pm, :], pm, pm == 0, (3,) if k == 0 else (2, 3))
-                quant(k + 1)
-                if k == 0:
-                    new_acc(2)
-                    plain(2, p_of[2][:, 0, :], 0, True)
-                if k >= 1:
-                    nc.vector.tensor_tensor(out=iu[:], in0=gi[:], in1=gu[:], op=ALU.mult)
-                if k >= 2:
-                    cols = slice((k - 2) * P, (k - 1) * P)
-                    nc.scalar.activation(out=tch[:, :, cols], in_=c_sb[:, :, cols], func=ACT.Tanh)
-                if k in (1, 3):
-                    tu(3 if k == 1 else 4, "s")
-                if 1 <= k < 3:
-                    nc.vector.tensor_tensor(out=c_sb[:, :, prev], in0=iu[:], in1=fc_sb[:, :, prev], op=ALU.add)
-
-            iu2 = iu
+            tw(1, 0, "s")
+            plain(1, p_of[1][:, 1, :], 1, False, (0, 1,))
+            tw(1, 1, "s")
+            order_pair(2)
+            tu(2, "s")
+            plain(1, p_of[1][:, 1, :], 1, False, (2,))
+            xt0 = x_tile()
+            mm_x(0, xt0)
+            x_out(0, xt0)
+            plain(1, p_of[1][:, 1, :], 1, False, (3,))
+            quant(1)
+            new_acc(2)
+            plain(2, p_of[2][:, 0, :], 0, True)
+            tw(2, 0, "s")
+            tw(2, 1, "s")
+            order_pair(3)
+            add_x(0)
+            gi0 = ep.tile([P, MT, P], F32, name="gi")
+            nc.scalar.activation(out=gi0[:], in_=p_of[0][:, :, 0:P], func=ACT.Sigmoid)
+            gu0 = ep.tile([P, MT, P], F32, name="gu")
+            nc.scalar.activation(out=gu0[:], in_=p_of[0][:, :, P:N], func=ACT.Tanh)
+            plain(2, p_of[2][:, 1, :], 1, False, (0, 1,))
+            xt1 = x_tile()
+            mm_x(1, xt1)
+            x_out(1, xt1)
+            plain(2, p_of[2][:, 1, :], 1, False, (2, 3,))
+            quant(2)
+            iu0 = ep.tile([P, MT, P], F32, name="iu")
+            nc.vector.tensor_tensor(out=iu0[:], in0=gi0[:], in1=gu0[:], op=ALU.mult)
+            tu(3, "s")
+            nc.vector.tensor_tensor(out=c_sb[:, :, 0 * P : 1 * P], in0=iu0[:], in1=fc_sb[:, :, 0 * P : 1 * P], op=ALU.add)
+            tw(3, 0, "s")
+            tw(3, 1, "s")
+            order_pair(4)
+            add_x(1)
+            gi1 = ep.tile([P, MT, P], F32, name="gi")
+            nc.scalar.activation(out=gi1[:], in_=p_of[1][:, :, 0:P], func=ACT.Sigmoid)
+            gu1 = ep.tile([P, MT, P], F32, name="gu")
+            nc.scalar.activation(out=gu1[:], in_=p_of[1][:, :, P:N], func=ACT.Tanh)
+            new_acc(3)
+            plain(3, p_of[3][:, 0, :], 0, True, (0, 1,))
+            xt2 = x_tile()
+            mm_x(2, xt2)
+            x_out(2, xt2)
+            plain(3, p_of[3][:, 0, :], 0, True, (2, 3,))
+            quant(3)
+            iu1 = ep.tile([P, MT, P], F32, name="iu")
+            nc.vector.tensor_tensor(out=iu1[:], in0=gi1[:], in1=gu1[:], op=ALU.mult)
+            nc.scalar.activation(out=tch[:, :, 0 * P : 1 * P], in_=c_sb[:, :, 0 * P : 1 * P], func=ACT.Tanh)
+            nc.vector.tensor_tensor(out=c_sb[:, :, 1 * P : 2 * P], in0=iu1[:], in1=fc_sb[:, :, 1 * P : 2 * P], op=ALU.add)
+            tw(4, 0, "s")
+            tw(4, 1, "s")
+            order_pair(5)
+            add_x(2)
+            gi2 = ep.tile([P, MT, P], F32, name="gi")
+            nc.scalar.activation(out=gi2[:], in_=p_of[2][:, :, 0:P], func=ACT.Sigmoid)
+            gu2 = ep.tile([P, MT, P], F32, name="gu")
+            nc.scalar.activation(out=gu2[:], in_=p_of[2][:, :, P:N], func=ACT.Tanh)
+            plain(3, p_of[3][:, 1, :], 1, False, (0, 1,))
+            xt3 = x_tile()
+            mm_x(3, xt3)
+            x_out(3, xt3)
+            plain(3, p_of[3][:, 1, :], 1, False, (2, 3,))
+            quant(4)
+            iu2 = ep.tile([P, MT, P], F32, name="iu")
+            nc.vector.tensor_tensor(out=iu2[:], in0=gi2[:], in1=gu2[:], op=ALU.mult)
+            nc.scalar.activation(out=tch[:, :, 1 * P : 2 * P], in_=c_sb[:, :, 1 * P : 2 * P], func=ACT.Tanh)
+            tu(4, "s")
             tw(5, 0, "s")
             tw(5, 1, "v")
             quant(5)
             add_x(3)
-            gi = ep.tile([P, MT, P], F32, name="gi")
-            nc.scalar.activation(out=gi[:], in_=p_of[3][:, :, 0:P], func=ACT.Sigmoid)
-            gu = ep.tile([P, MT, P], F32, name="gu")
-            nc.scalar.activation(out=gu[:], in_=p_of[3][:, :, P:N], func=ACT.Tanh)
+            gi3 = ep.tile([P, MT, P], F32, name="gi")
+            nc.scalar.activation(out=gi3[:], in_=p_of[3][:, :, 0:P], func=ACT.Sigmoid)
+            gu3 = ep.tile([P, MT, P], F32, name="gu")
+            nc.scalar.activation(out=gu3[:], in_=p_of[3][:, :, P:N], func=ACT.Tanh)
             tu(5, "s")
             new_acc(4)
             plain(4, p_of[4][:, 0, :], 0, True)
-            xt = x_tile()
-            mm_x(4, xt)
-            iu = ep.tile([P, MT, P], F32, name="iu")
-            nc.vector.tensor_tensor(out=iu[:], in0=gi[:], in1=gu[:], op=ALU.mult)
+            xt4 = x_tile()
+            mm_x(4, xt4)
+            iu3 = ep.tile([P, MT, P], F32, name="iu")
+            nc.vector.tensor_tensor(out=iu3[:], in0=gi3[:], in1=gu3[:], op=ALU.mult)
             nc.vector.tensor_tensor(out=c_sb[:, :, 2 * P : 3 * P], in0=iu2[:], in1=fc_sb[:, :, 2 * P : 3 * P], op=ALU.add)
-            nc.vector.tensor_tensor(out=c_sb[:, :, 3 * P : CH], in0=iu[:], in1=fc_sb[:, :, 3 * P : CH], op=ALU.add)
+            nc.vector.tensor_tensor(out=c_sb[:, :, 3 * P : 4 * P], in0=iu3[:], in1=fc_sb[:, :, 3 * P : 4 * P], op=ALU.add)
             xs_of[4] = ep.tile([P, NB, MT * P], F32, name="xs")
-            x_out_half(4, xt, 0, "s")
-            x_out_half(4, xt, 1, "s")
+            x_out_half(4, xt4, 0, "s")
+            x_out_half(4, xt4, 1, "s")
             plain(4, p_of[4][:, 1, :], 1, False)
             nc.sync.dma_start(out=out0v[:, :, CH : 2 * CH], in_=c_sb[:])
             p5 = [psP.tile([P, N], F32, name="p5_0", tag="P"), psT.tile([P, N], F32, name="p5_1", tag="T")]
-            xt = psT.tile([P, NB, MT * P], F32, name="xt5", tag="T")
-            mm_x(LAST, xt)
-            xs_of[LAST] = ep.tile([P, NB, MT * P], F32, name="xs")
-            x_out_half(LAST, xt, 0, "s")
-            x_out_half(LAST, xt, 1, "s")
+            xt5 = psT.tile([P, NB, MT * P], F32, name="xt5", tag="T")
+            mm_x(5, xt5)
+            xs_of[5] = ep.tile([P, NB, MT * P], F32, name="xs")
+            x_out_half(5, xt5, 0, "s")
+            x_out_half(5, xt5, 1, "s")
             absmax(0, 0, 2 * P)
             absmax(1, 2 * P, CH)
             add_x(4)

@@ -337,11 +337,11 @@ def tile_treelstm_pb_kernel(
             quant(2)
             iu0 = ep.tile([P, MT, P], F32, name="iu")
             nc.vector.tensor_tensor(out=iu0[:], in0=gi0[:], in1=gu0[:], op=ALU.mult)
+            order_pair(4)
             tu(3, "s")
             nc.vector.tensor_tensor(out=c_sb[:, :, 0 * P : 1 * P], in0=iu0[:], in1=fc_sb[:, :, 0 * P : 1 * P], op=ALU.add)
             tw(3, 0, "s")
             tw(3, 1, "s")
-            order_pair(4)
             add_x(1)
             gi1 = ep.tile([P, MT, P], F32, name="gi")
             nc.scalar.activation(out=gi1[:], in_=p_of[1][:, :, 0:P], func=ACT.Sigmoid)
@@ -356,11 +356,11 @@ def tile_treelstm_pb_kernel(
             quant(3)
             iu1 = ep.tile([P, MT, P], F32, name="iu")
             nc.vector.tensor_tensor(out=iu1[:], in0=gi1[:], in1=gu1[:], op=ALU.mult)
+            order_pair(5)
             nc.scalar.activation(out=tch[:, :, 0 * P : 1 * P], in_=c_sb[:, :, 0 * P : 1 * P], func=ACT.Tanh)
             nc.vector.tensor_tensor(out=c_sb[:, :, 1 * P : 2 * P], in0=iu1[:], in1=fc_sb[:, :, 1 * P : 2 * P], op=ALU.add)
             tw(4, 0, "s")
             tw(4, 1, "s")
-            order_pair(5)
             add_x(2)
             gi2 = ep.tile([P, MT, P], F32, name="gi")
             nc.scalar.activation(out=gi2[:], in_=p_of[2][:, :, 0:P], func=ACT.Sigmoid)

@@ -94,11 +94,11 @@ def tile_treelstm_pb_kernel(
         load_w(2)
         load_w(3)
         load_u(3)
+        load_w(4)
         fc_sb = inp.tile([P, MT, CH], BF16, name="fc_sb")
         nc.sync.dma_start(out=fc_sb[:], in_=fc_sum.rearrange("(p m) c -> p m c", p=P))
-        load_w(4)
-        u_in[NA] = load_rows(U_o, 0, NB, CH, "Uo0")
         load_w(5)
+        u_in[NA] = load_rows(U_o, 0, NB, CH, "Uo0")
         u_in[NA + 1] = load_rows(U_o, NB, NB, CH, "Uo1")
 
         hT = keep.tile([P, MT, KT, P], BF16, name="hT")
@@ -404,8 +404,7 @@ def tile_treelstm_pb_kernel(
             xs_of[5] = ep.tile([P, NB, MT * P], F32, name="xs")
             x_out_half(5, xt5, 0, "s")
             x_out_half(5, xt5, 1, "s")
-            absmax(0, 0, 2 * P)
-            absmax(1, 2 * P, CH)
+            absmax(0, 0, CH)
             add_x(4)
             plain(LAST, p5[0][:], 0, True)
             go4 = ep.tile([P, MT, N], F32, name="go4", bufs=1)
@@ -415,13 +414,10 @@ def tile_treelstm_pb_kernel(
                 func=ACT.Sigmoid,
             )
             nc.scalar.activation(out=tch[:, :, 2 * P : CH], in_=c_sb[:, :, 2 * P : CH], func=ACT.Tanh)
-            nc.vector.tensor_scalar(out=sab[:], in0=pmx[:, 0, :], scalar1=1.0 / 448.0, scalar2=None, op0=ALU.mult)
             t_add(p5[0][:], xs_of[LAST], 0, True)
             plain(LAST, p5[1][:], 1, True)
             t_add(p5[1][:], xs_of[LAST], 1, True)
-            nc.vector.scalar_tensor_tensor(
-                out=sc[:], in0=pmx[:, 1, :], scalar=1.0 / 448.0, in1=sab[:], op0=ALU.mult, op1=ALU.max
-            )
+            nc.vector.tensor_scalar(out=sc[:], in0=pmx[:, 0, :], scalar1=1.0 / 448.0, scalar2=None, op0=ALU.mult)
             nc.vector.tensor_tensor(out=h_sb[:, :, 0:N], in0=go4[:], in1=tch[:, :, 0:N], op=ALU.mult)
             nc.sync.dma_start(out=out0v[:, :, 0:N], in_=h_sb[:, :, 0:N])
             go5 = [ep.tile([P, N], F32, name="go5_%d" % m, bufs=1) for m in range(MT)]

from contextlib import ExitStack

import concourse.mybir as mybir
from concourse.masks import make_identity

B, SIZE, CH = 256, 1024, 512
FLOPS = 2 * B * (3 * CH) * (SIZE + CH)

F32 = mybir.dt.float32
BF16 = mybir.dt.bfloat16
U32 = mybir.dt.uint32
U8 = mybir.dt.uint8
FP8X4 = mybir.dt.float8_e4m3fn_x4
FP8 = mybir.dt.float8_e4m3fn
ACT = mybir.ActivationFunctionType
ALU = mybir.AluOpType
AX = mybir.AxisListType

P = 128
MT = B // P
KT = CH // P
NPASS = SIZE // 512
NB = 2
N = NB * P
NA = 4
NS = 6
LAST = NS - 1


def tile_treelstm_pb_kernel(
    tc, z0, h_tilde, fc_sum, W_i, U_i, b_i, W_o, U_o, b_o, W_u, U_u, b_u, out_0, out_1
):
    nc = tc.nc
    out0v = out_0.rearrange("(p m) n -> p m n", p=P)
    out1v = out_1.rearrange("(p m) n -> p m n", p=P)

    with ExitStack() as ctx:
        const = ctx.enter_context(tc.tile_pool(name="const", bufs=1))
        inp = ctx.enter_context(tc.tile_pool(name="inp", bufs=1))
        keep = ctx.enter_context(tc.tile_pool(name="keep", bufs=1))
        ep = ctx.enter_context(tc.tile_pool(name="ep", bufs=3))
        psT = ctx.enter_context(tc.psum_pool(name="psT", bufs=4))
        psP = ctx.enter_context(tc.psum_pool(name="psP", bufs=3))
        psX = ctx.enter_context(tc.psum_pool(name="psX", bufs=1))

        ones = const.tile([P, CH], BF16, name="ones")
        nc.vector.memset(ones[:].bitcast(mybir.dt.int32), 0x3F803F80)
        bias_rows = const.tile([P, P], BF16, name="bias_rows")
        nc.vector.memset(bias_rows[:], 0.0)
        bo_rows = const.tile([P, N], BF16, name="bo_rows")
        nc.vector.memset(bo_rows[:], 0.0)
        zcol = const.tile([P, 1], F32, name="zcol")
        nc.vector.memset(zcol[:], 0.0)
        warm = const.tile([P, 1], F32, name="warm")
        nc.scalar.activation(out=warm[:], in_=zcol[:], func=ACT.Sigmoid)
        ident_b = const.tile([P, P], BF16, name="ident_b")
        make_identity(nc, ident_b[:])
        ident_f = const.tile([P, P], F32, name="ident_f")
        make_identity(nc, ident_f[:])

        def load_rows(dram, r0, nrt, width, name):
            t = inp.tile([P, nrt, width], BF16, name=name)
            nc.sync.dma_start(
                out=t[:], in_=dram[r0 * P : (r0 + nrt) * P, :].rearrange("(p t) k -> p t k", p=P)
            )
            return [t[:, j, :] for j in range(nrt)]

        u_in = {}
        w_in = {}

        def load_w(k):
            t = inp.tile([P, NB, SIZE], BF16, name="W%d" % k)
            if k < NA:
                for j, W in enumerate((W_i, W_u)):
                    nc.sync.dma_start(out=t[:, j, :], in_=W[k * P : (k + 1) * P, :])
            else:
                r0 = (k - NA) * N
                nc.sync.dma_start(out=t[:], in_=W_o[r0 : r0 + N, :].rearrange("(p t) k -> p t k", p=P))
            w_in[k] = t

        def load_u(k):
            u_in[k] = load_rows(U_i, k, 1, CH, "Ui%d" % k) + load_rows(U_u, k, 1, CH, "Uu%d" % k)

        h_in = load_rows(h_tilde, 0, MT, CH, "h_in")
        load_u(0)
        load_u(1)
        z_in = load_rows(z0, 0, MT, SIZE, "z_in")
        load_w(0)
        for j, b in enumerate((b_i, b_u)):
            nc.sync.dma_start(out=bias_rows[j * KT : (j + 1) * KT, :], in_=b.rearrange("(t c) -> t c", c=P))
        nc.sync.dma_start(out=bo_rows[0:2, :], in_=b_o.rearrange("(s c) -> s c", c=N))
        load_w(1)
        load_u(2)
        load_w(2)
        load_w(3)
        load_u(3)
        load_w(4)
        fc_sb = inp.tile([P, MT, CH], BF16, name="fc_sb")
        nc.sync.dma_start(out=fc_sb[:], in_=fc_sum.rearrange("(p m) c -> p m c", p=P))
        load_w(5)
        u_in[NA] = load_rows(U_o, 0, NB, CH, "Uo0")
        u_in[NA + 1] = load_rows(U_o, NB, NB, CH, "Uo1")

        hT = keep.tile([P, MT, KT, P], BF16, name="hT")
        zgr = keep.tile([P, NPASS * MT * P * 4], BF16, name="zgr", align_bytes=64)
        zc = keep.tile([P, NPASS * MT * P], U32, name="zc", align_bytes=64)
        zs = keep.tile([P, NPASS * MT * P], U8, name="zs", align_bytes=64)
        bias_sb = keep.tile([P, NS, NB], F32, name="bias_sb")
        c_sb = keep.tile([P, MT, CH], F32, name="c_sb")
        tch = keep.tile([P, MT, CH], F32, name="tch")
        h_sb = keep.tile([P, MT, CH], F32, name="h_sb")
        pmx = keep.tile([P, 3, MT], F32, name="pmx")
        mab = keep.tile([P, MT], F32, name="mab")
        sab = keep.tile([P, MT], F32, name="sab")
        sc = keep.tile([P, MT], F32, name="sc")
        rs = keep.tile([P, MT], F32, name="rs")
        qc = keep.tile([P, MT, CH], FP8, name="qc")
        qh = keep.tile([P, MT, CH], FP8, name="qh")
        uT = [keep.tile([P, 2, N, 2], BF16, name="uT%d" % k) for k in range(NS)]
        wo = {k: keep.tile([P, NB, NPASS, 2, P], F32, name="wo%d" % k) for k in [0,2,3,4,5]}
        zo = keep.tile([P, MT, NPASS, 2, P], F32, name="zo")
        wgr = [keep.tile([P, NPASS * N * 4], BF16, name="wgr%d" % k, align_bytes=64) for k in range(NS)]
        wc = [keep.tile([P, NPASS * N], U32, name="wc%d" % k, align_bytes=64) for k in range(NS)]
        ws = [keep.tile([P, NPASS * N], U8, name="ws%d" % k, align_bytes=64) for k in range(NS)]

        def copy_out(eng, out, in_):
            if eng == "v":
                nc.vector.tensor_copy(out=out, in_=in_)
            else:
                nc.scalar.copy(out=out, in_=in_)

        def t_h(m, eng):
            pt = psT.tile([P, KT, P], BF16, name="pt", tag="T")
            for kt in range(KT):
                j, e = divmod(kt, 2)
                nc.tensor.transpose(pt[:, kt, :], h_in[m][:, 256 * j + e : 256 * (j + 1) : 2], ident_b[:])
            copy_out(eng, hT[:, m], pt[:])

        def word_view(t):
            return t[:].bitcast(F32).rearrange("p (g c u) -> p g c u", g=NPASS, u=2)

        def order_words(t, j, src, eng):
            copy_out(
                eng,
                t[:, j].rearrange("p g u q -> p g u q"),
                src.bitcast(F32).rearrange("p (g q u) -> p g u q", g=NPASS, u=2),
            )

        def order_pair(k):
            nc.vector.tensor_copy(
                out=wo[k][:].rearrange("p j g u q -> p (j g) u q"),
                in_=w_in[k][:].bitcast(F32).rearrange("p j (g q u) -> p (j g) u q", g=NPASS, u=2),
            )

        def t_words(words, dst, eng):
            pw = psT.tile([P, NPASS, 2, P], F32, name="pw", tag="T")
            for g in range(NPASS):
                for u in range(2):
                    nc.tensor.transpose(pw[:, g, u, :], words(g, u), ident_f[:])
            copy_out(eng, dst, pw[:].rearrange("p g u c -> p g c u"))

        def stepped(src):
            w = src.bitcast(F32)
            return lambda g, u: w[:, 256 * g + u : 256 * (g + 1) : 2]

        def ordered(t, j):
            return lambda g, u: t[:, j, g, u, :]

        def tz(m, eng):
            dst = word_view(zgr)[:, :, m * P : (m + 1) * P, :]
            t_words(ordered(zo, m) if True else stepped(z_in[m]), dst, eng)

        def tw(k, j, eng):
            dst = word_view(wgr[k])[:, :, j * P : (j + 1) * P, :]
            t_words(ordered(wo[k], j) if k in wo else stepped(w_in[k][:, j, :]), dst, eng)

        def tu_half(k, b, eng):
            pu = psT.tile([P, 2, P], F32, name="pu_half", tag="T")
            words = u_in[k][b].bitcast(F32)
            for j in range(2):
                nc.tensor.transpose(pu[:, j, :], words[:, j * P : (j + 1) * P], ident_f[:])
            dst = uT[k][:].rearrange("p j c e -> p (j c e)").bitcast(F32).rearrange("p (j b c) -> p j b c", j=2, b=NB)
            copy_out(eng, dst[:, :, b, :], pu[:])

        def tu(k, eng):
            pu = psT.tile([P, NB, 2, P], F32, name="pu", tag="T")
            for b in range(NB):
                words = u_in[k][b].bitcast(F32)
                for j in range(2):
                    nc.tensor.transpose(pu[:, b, j, :], words[:, j * P : (j + 1) * P], ident_f[:])
            dst = uT[k][:].rearrange("p j c e -> p (j c e)").bitcast(F32).rearrange("p (j b c) -> p j b c", j=2, b=NB)
            copy_out(eng, dst, pu[:].rearrange("p b j c -> p j b c"))

        def quant(k):
            nc.vector.quantize_mx(out=wc[k][:].bitcast(FP8X4), scales=ws[k][:], in_=wgr[k][:])

        def mm_p(k, out, m, kt, start):
            nc.tensor.matmul(
                out=out, lhsT=hT[:, m, kt, :], rhs=uT[k][:, kt // 2, :, kt % 2], start=start, stop=False
            )

        def mm_x(k, xt):
            for j in range(NB):
                for g in range(NPASS):
                    zcols = slice(g * MT * P, (g + 1) * MT * P)
                    wcols = slice(g * N + j * P, g * N + (j + 1) * P)
                    nc.tensor.matmul_mx(
                        out=xt[:, j, :],
                        lhsT=wc[k][:, wcols].bitcast(FP8X4),
                        lhsT_scale=ws[k][:, wcols],
                        rhs=zc[:, zcols].bitcast(FP8X4),
                        rhs_scale=zs[:, zcols],
                        start=(g == 0),
                        stop=(g == NPASS - 1),
                    )

        def x_bias(k):
            return bias_sb[:, k, :]

        def x_out(k, xt):
            xs_of[k] = ep.tile([P, NB, MT * P], F32, name="xs")
            nc.vector.tensor_tensor(
                out=xs_of[k][:], in0=xt[:], in1=x_bias(k).unsqueeze(2).to_broadcast([P, NB, MT * P]), op=ALU.add
            )

        def x_out_half(k, xt, j, eng):
            b = x_bias(k)[:, j : j + 1]
            if eng == "v":
                nc.vector.tensor_scalar(
                    out=xs_of[k][:, j, :], in0=xt[:, j, :], scalar1=b, scalar2=None, op0=ALU.add
                )
            else:
                nc.scalar.activation(out=xs_of[k][:, j, :], in_=xt[:, j, :], func=ACT.Identity, bias=b)

        def t_add(out, xs, m, stop):
            for j in range(NB):
                nc.tensor.matmul(
                    out=out[:, j * P : (j + 1) * P],
                    lhsT=xs[:, j, m * P : (m + 1) * P],
                    rhs=ident_f[:],
                    start=False,
                    stop=(stop and j == NB - 1),
                    is_transpose=True,
                )

        def absmax(j, lo, hi):
            for m in range(MT):
                nc.vector.tensor_reduce(
                    out=pmx[:, j, m : m + 1], in_=c_sb[:, m, lo:hi], axis=AX.X, op=ALU.max, apply_absolute_value=True
                )

        def cast(eng, out, in_, m):
            if eng == "v":
                nc.vector.tensor_scalar(
                    out=out, in0=in_, scalar1=rs[:, m : m + 1], scalar2=None, op0=ALU.mult, saturate=False
                )
            else:
                nc.scalar.activation(
                    out=out, in_=in_, func=ACT.Identity, scale=rs[:, m : m + 1], bias=zcol[:, 0:1], saturate=False
                )

        def plain(k, out, m, start, kts=range(KT)):
            for kt in kts:
                mm_p(k, out, m, kt, start and kt == 0)

        p_of = {}
        xs_of = {}

        def new_acc(k):
            p_of[k] = psP.tile([P, MT, N], F32, name="acc", tag="P")

        def x_tile():
            return psX.tile([P, NB, MT * P], F32, name="xt", tag="X")

        def add_x(k):
            for m in range(MT):
                t_add(p_of[k][:, m, :], xs_of[k], m, m == MT - 1)

        with tc.manual_schedule():
            warm_ps = psT.tile([P, CH], F32, name="warm_ps", tag="T")
            for i in range(3):
                nc.tensor.matmul(out=warm_ps[:], lhsT=ones[:, 0:P], rhs=ones[:], start=True, stop=True)
            t_h(0, "v")
            tu_half(0, 0, "v")
            tu_half(0, 1, "s")
            t_h(1, "v")
            tu(1, "s")
            new_acc(0)
            plain(0, p_of[0][:, 0, :], 0, True)
            plain(0, p_of[0][:, 1, :], 1, False)
            order_words(zo, 0, z_in[0], "v")
            order_words(zo, 1, z_in[1], "v")
            order_words(wo[0], 0, w_in[0][:, 0, :], "s")
            tz(0, "v")
            tz(1, "s")
            order_words(wo[0], 1, w_in[0][:, 1, :], "v")
            new_acc(1)
            plain(1, p_of[1][:, 0, :], 0, True, (0, 1))
            tw(0, 0, "v")
            plain(1, p_of[1][:, 0, :], 0, True, (2, 3))
            tw(0, 1, "s")
            pbias = psT.tile([P, 3, P], BF16, name="pbias", tag="T")
            nc.tensor.transpose(pbias[:, 0, :], bias_rows[:], ident_b[:])
            for j in range(NB):
                nc.tensor.transpose(pbias[:, 1 + j, :], bo_rows[:, j:N:2], ident_b[:])
            nc.scalar.copy(out=bias_sb[:, 0:NA, :], in_=pbias[:, 0, 0 : NB * KT].rearrange("p (g t) -> p t g", g=NB))
            nc.scalar.copy(out=bias_sb[:, NA:NS, :], in_=pbias[:, 1 : 1 + NB, 0 : NS - NA].rearrange("p j s -> p s j"))
            nc.vector.quantize_mx(out=zc[:].bitcast(FP8X4), scales=zs[:], in_=zgr[:])
            quant(0)

            tw(1, 0, "s")
            plain(1, p_of[1][:, 1, :], 1, False, (0, 1,))
            tw(1, 1, "s")
            order_pair(2)
            tu(2, "s")
            plain(1, p_of[1][:, 1, :], 1, False, (2,))
            xt0 = x_tile()
            mm_x(0, xt0)
            x_out(0, xt0)
            plain(1, p_of[1][:, 1, :], 1, False, (3,))
            quant(1)
            new_acc(2)
            plain(2, p_of[2][:, 0, :], 0, True)
            tw(2, 0, "s")
            tw(2, 1, "s")
            order_pair(3)
            add_x(0)
            gi0 = ep.tile([P, MT, P], F32, name="gi")
            nc.scalar.activation(out=gi0[:], in_=p_of[0][:, :, 0:P], func=ACT.Sigmoid)
            gu0 = ep.tile([P, MT, P], F32, name="gu")
            nc.scalar.activation(out=gu0[:], in_=p_of[0][:, :, P:N], func=ACT.Tanh)
            plain(2, p_of[2][:, 1, :], 1, False, (0, 1,))
            xt1 = x_tile()
            mm_x(1, xt1)
            x_out(1, xt1)
            plain(2, p_of[2][:, 1, :], 1, False, (2, 3,))
            quant(2)
            iu0 = ep.tile([P, MT, P], F32, name="iu")
            nc.vector.tensor_tensor(out=iu0[:], in0=gi0[:], in1=gu0[:], op=ALU.mult)
            order_pair(4)
            tu(3, "s")
            nc.vector.tensor_tensor(out=c_sb[:, :, 0 * P : 1 * P], in0=iu0[:], in1=fc_sb[:, :, 0 * P : 1 * P], op=ALU.add)
            tw(3, 0, "s")
            tw(3, 1, "s")
            add_x(1)
            gi1 = ep.tile([P, MT, P], F32, name="gi")
            nc.scalar.activation(out=gi1[:], in_=p_of[1][:, :, 0:P], func=ACT.Sigmoid)
            gu1 = ep.tile([P, MT, P], F32, name="gu")
            nc.scalar.activation(out=gu1[:], in_=p_of[1][:, :, P:N], func=ACT.Tanh)
            new_acc(3)
            plain(3, p_of[3][:, 0, :], 0, True, (0, 1,))
            xt2 = x_tile()
            mm_x(2, xt2)
            x_out(2, xt2)
            plain(3, p_of[3][:, 0, :], 0, True, (2, 3,))
            quant(3)
            iu1 = ep.tile([P, MT, P], F32, name="iu")
            nc.vector.tensor_tensor(out=iu1[:], in0=gi1[:], in1=gu1[:], op=ALU.mult)
            order_pair(5)
            nc.scalar.activation(out=tch[:, :, 0 * P : 1 * P], in_=c_sb[:, :, 0 * P : 1 * P], func=ACT.Tanh)
            nc.vector.tensor_tensor(out=c_sb[:, :, 1 * P : 2 * P], in0=iu1[:], in1=fc_sb[:, :, 1 * P : 2 * P], op=ALU.add)
            tw(4, 0, "s")
            tw(4, 1, "s")
            add_x(2)
            gi2 = ep.tile([P, MT, P], F32, name="gi")
            nc.scalar.activation(out=gi2[:], in_=p_of[2][:, :, 0:P], func=ACT.Sigmoid)
            gu2 = ep.tile([P, MT, P], F32, name="gu")
            nc.scalar.activation(out=gu2[:], in_=p_of[2][:, :, P:N], func=ACT.Tanh)
            plain(3, p_of[3][:, 1, :], 1, False, (0, 1,))
            xt3 = x_tile()
            mm_x(3, xt3)
            x_out(3, xt3)
            plain(3, p_of[3][:, 1, :], 1, False, (2, 3,))
            quant(4)
            iu2 = ep.tile([P, MT, P], F32, name="iu")
            nc.vector.tensor_tensor(out=iu2[:], in0=gi2[:], in1=gu2[:], op=ALU.mult)
            nc.scalar.activation(out=tch[:, :, 1 * P : 2 * P], in_=c_sb[:, :, 1 * P : 2 * P], func=ACT.Tanh)
            tu(4, "s")
            tw(5, 0, "s")
            tw(5, 1, "v")
            quant(5)
            add_x(3)
            gi3 = ep.tile([P, MT, P], F32, name="gi")
            nc.scalar.activation(out=gi3[:], in_=p_of[3][:, :, 0:P], func=ACT.Sigmoid)
            gu3 = ep.tile([P, MT, P], F32, name="gu")
            nc.scalar.activation(out=gu3[:], in_=p_of[3][:, :, P:N], func=ACT.Tanh)
            tu(5, "s")
            new_acc(4)
            plain(4, p_of[4][:, 0, :], 0, True)
            xt4 = x_tile()
            mm_x(4, xt4)
            iu3 = ep.tile([P, MT, P], F32, name="iu")
            nc.vector.tensor_tensor(out=iu3[:], in0=gi3[:], in1=gu3[:], op=ALU.mult)
            nc.vector.tensor_tensor(out=c_sb[:, :, 2 * P : 3 * P], in0=iu2[:], in1=fc_sb[:, :, 2 * P : 3 * P], op=ALU.add)
            nc.vector.tensor_tensor(out=c_sb[:, :, 3 * P : 4 * P], in0=iu3[:], in1=fc_sb[:, :, 3 * P : 4 * P], op=ALU.add)
            xs_of[4] = ep.tile([P, NB, MT * P], F32, name="xs")
            x_out_half(4, xt4, 0, "s")
            x_out_half(4, xt4, 1, "s")
            plain(4, p_of[4][:, 1, :], 1, False)
            nc.sync.dma_start(out=out0v[:, :, CH : 2 * CH], in_=c_sb[:])
            p5 = [psP.tile([P, N], F32, name="p5_0", tag="P"), psT.tile([P, N], F32, name="p5_1", tag="T")]
            xt5 = psT.tile([P, NB, MT * P], F32, name="xt5", tag="T")
            mm_x(5, xt5)
            xs_of[5] = ep.tile([P, NB, MT * P], F32, name="xs")
            x_out_half(5, xt5, 0, "s")
            x_out_half(5, xt5, 1, "s")
            absmax(0, 0, CH)
            add_x(4)
            plain(LAST, p5[0][:], 0, True)
            go4 = ep.tile([P, MT, N], F32, name="go4", bufs=1)
            nc.scalar.activation(
                out=go4[:].rearrange("p m (q j) -> p m q j", j=NB),
                in_=p_of[4][:].rearrange("p m (j q) -> p m q j", j=NB),
                func=ACT.Sigmoid,
            )
            nc.scalar.activation(out=tch[:, :, 2 * P : CH], in_=c_sb[:, :, 2 * P : CH], func=ACT.Tanh)
            t_add(p5[0][:], xs_of[LAST], 0, True)
            plain(LAST, p5[1][:], 1, True)
            t_add(p5[1][:], xs_of[LAST], 1, True)
            nc.vector.tensor_scalar(out=sc[:], in0=pmx[:, 0, :], scalar1=1.0 / 448.0, scalar2=None, op0=ALU.mult)
            nc.vector.tensor_tensor(out=h_sb[:, :, 0:N], in0=go4[:], in1=tch[:, :, 0:N], op=ALU.mult)
            nc.sync.dma_start(out=out0v[:, :, 0:N], in_=h_sb[:, :, 0:N])
            go5 = [ep.tile([P, N], F32, name="go5_%d" % m, bufs=1) for m in range(MT)]
            for m in range(MT):
                nc.scalar.activation(
                    out=go5[m][:].rearrange("p (q j) -> p q j", j=NB),
                    in_=p5[m][:].rearrange("p (j q) -> p q j", j=NB),
                    func=ACT.Sigmoid,
                )
            nc.vector.reciprocal(out=rs[:], in_=sc[:])
            for m in range(MT):
                nc.vector.tensor_tensor(out=h_sb[:, m, N:CH], in0=go5[m][:], in1=tch[:, m, N:CH], op=ALU.mult)
            nc.sync.dma_start(out=out0v[:, :, N:CH], in_=h_sb[:, :, N:CH])
            for m in range(MT):
                cast("s", qc[:, m, :], c_sb[:, m, :], m)
            nc.sync.dma_start(out=out1v[:, :, CH : 2 * CH], in_=qc[:].bitcast(U8))
            for m in range(MT):
                cast("v", qh[:, m, :], h_sb[:, m, :], m)
            nc.sync.dma_start(out=out1v[:, :, 0:CH], in_=qh[:].bitcast(U8))
